import numpy as np
import ml_dtypes


def mxq(x, axis, fmt="e4m3"):
    dtype, down = {"e4m3": (ml_dtypes.float8_e4m3fn, 7), "e5m2": (ml_dtypes.float8_e5m2, 14)}[fmt]
    v = np.moveaxis(np.asarray(x, np.float32).astype(ml_dtypes.bfloat16).astype(np.float64), axis, -1)
    blocks = v.reshape(v.shape[:-1] + (-1, 32))
    amax = np.abs(blocks).max(-1, keepdims=True)
    byte = np.maximum(np.where(amax > 0, np.frexp(amax)[1] - 1 + 127, 0) - down, 1)
    scale = np.exp2(byte - 127.0)
    codes = (blocks / scale).astype(np.float32).astype(dtype).astype(np.float64)
    return np.moveaxis((codes * scale).reshape(v.shape), -1, axis)


WIDE = False


def mx_kscale(k):
    if not WIDE:
        return np.ones(k)
    levels = np.array([10, -10, 5, -5, 0])
    a = np.random.permutation(np.resize(levels, k // 512 * 4)).reshape(k // 512, 4)
    idx = np.arange(k)
    return np.exp2(a[idx // 512, idx % 128 // 32])


BF16 = ml_dtypes.bfloat16


def bf(x):
    return np.asarray(x, np.float32).astype(BF16)


def f64(x):
    return np.asarray(x).astype(np.float64)


B, N, D, DH, BI, BJ = 1, 512, 128, 128, 128, 64
EPS = 1e-5
KEEP = 0.85


def layer_norm(v, w, b):
    m = v.mean(-1, keepdims=True)
    vc = v - m
    inv = 1.0 / np.sqrt((vc * vc).mean(-1, keepdims=True) + EPS)
    return vc * inv * w + b


def setup_inputs():
    s = mx_kscale(N)[None, :, None]
    return {"a_gated": bf(np.random.standard_normal((BI, N, DH)) * 0.5 * s),
            "b_gated": bf(np.random.standard_normal((BJ, N, DH)) * 0.5 / s),
            "mask": bf(np.random.random((BI, N)) < KEEP),
            "norm_out_w": bf(1.0 + 0.1 * np.random.standard_normal(DH)),
            "norm_out_b": bf(0.1 * np.random.standard_normal(DH))}


def reference(a_gated, b_gated, mask, norm_out_w, norm_out_b):
    am = f64(a_gated) * f64(mask)[:, :, None]
    t = mxq(am.transpose(2, 0, 1), 2, "e4m3") @ mxq(f64(b_gated).transpose(2, 1, 0), 1, "e4m3")
    return layer_norm(t.transpose(1, 2, 0), f64(norm_out_w), f64(norm_out_b))

@@ -1,0 +1,187 @@
+from contextlib import ExitStack
+
+import concourse.mybir as mybir
+from concourse.masks import make_identity
+
+FP8X4 = mybir.dt.float8_e4m3fn_x4
+BF16 = mybir.dt.bfloat16
+F32 = mybir.dt.float32
+U32 = mybir.dt.uint32
+U8 = mybir.dt.uint8
+ALU = mybir.AluOpType
+ACT = mybir.ActivationFunctionType
+
+P = 128
+PACK = 4
+NI, NJ, NK, ND = 128, 64, 512, 128
+EPS = 1e-5
+FLOPS = 2 * NI * NJ * NK * ND
+
+ROWS = 64
+CH = 8
+NCH = ROWS // CH
+DQ = 32
+NQ = ND // DQ
+DBANK = 8
+JH = 32
+JB = 16
+
+SCALAR_Q_A = (0, 1, 2)
+SCALAR_Q_B = (0, 1)
+
+
+def tile_trianglemultiplication_pa_kernel(tc, a_gated, b_gated, mask, norm_out_w, norm_out_b, out):
+    nc = tc.nc
+    with ExitStack() as ctx:
+        keep = ctx.enter_context(tc.tile_pool(name="keep", bufs=1))
+        small = ctx.enter_context(tc.tile_pool(name="small", bufs=1))
+        rawp = ctx.enter_context(tc.tile_pool(name="rawp", bufs=3))
+        grp = ctx.enter_context(tc.tile_pool(name="grp", bufs=5))
+        psum = ctx.enter_context(tc.psum_pool(name="psum", bufs=8))
+
+        a_codes = keep.tile([P, ND, NI], U32, align_bytes=64)
+        a_scales = keep.tile([P, ND, NI], U8, align_bytes=64)
+        b_codes = keep.tile([P, ND, NJ], U32, align_bytes=64)
+        b_scales = keep.tile([P, ND, NJ], U8, align_bytes=64)
+
+        eps_t = small.tile([P, 1], F32)
+        nc.vector.memset(eps_t[:], EPS)
+        warm = small.tile([P, 1], F32)
+        nc.scalar.activation(out=warm[:], in_=eps_t[:], func=ACT.Sqrt)
+
+        ident = small.tile([P, P], BF16)
+        make_identity(nc, ident[:])
+        mask_ik = small.tile([P, NK], BF16)
+        nc.sync.dma_start(out=mask_ik[:], in_=mask)
+        mask_itp = small.tile([P, PACK, P], BF16)
+        nc.vector.tensor_copy(out=mask_itp[:], in_=mask_ik[:].rearrange("i (p t) -> i t p", t=PACK))
+        mask_ps = psum.tile([P, PACK, P], BF16, tag="bank")
+        for t in range(PACK):
+            nc.tensor.transpose(mask_ps[:, t, :], mask_itp[:, t, :], ident[:])
+        mask_pit = small.tile([P, NI, PACK], BF16)
+        nc.vector.tensor_copy(out=mask_pit[:], in_=mask_ps[:].rearrange("p t i -> p i t"))
+
+        wb16 = small.tile([P, 2, ND], BF16)
+        nc.scalar.dma_start(out=wb16[:, 0, :], in_=norm_out_w.partition_broadcast(P))
+        nc.scalar.dma_start(out=wb16[:, 1, :], in_=norm_out_b.partition_broadcast(P))
+        wb = small.tile([P, 2, ND], F32)
+        nc.vector.tensor_copy(out=wb[:], in_=wb16[:])
+
+        groups = ((a_gated, 0, True), (a_gated, ROWS, True), (b_gated, 0, False))
+        for gi, (src, row0, is_a) in enumerate(groups):
+            on_scalar = SCALAR_Q_A if is_a else SCALAR_Q_B
+            g = [
+                grp.tile([P, DQ, ROWS, PACK], BF16, tag="g", name="g%d_%d" % (gi, q), align_bytes=64)
+                for q in range(NQ)
+            ]
+            for c in range(NCH):
+                r0 = row0 + c * CH
+                raw = rawp.tile([P, CH, PACK, ND], BF16, tag="raw")
+                nc.sync.dma_start(
+                    out=raw[:].rearrange("p r t d -> p r (t d)"),
+                    in_=src[r0 : r0 + CH].rearrange("r (p t) d -> p r (t d)", t=PACK),
+                )
+                for q in range(NQ):
+                    dst = g[q][:, :, c * CH : (c + 1) * CH, :]
+                    view = raw[:, :, :, q * DQ : (q + 1) * DQ].rearrange("p r t d -> p d r t")
+                    if q in on_scalar:
+                        nc.scalar.copy(out=dst, in_=view)
+                    elif is_a:
+                        nc.vector.tensor_tensor(
+                            out=dst,
+                            in0=view,
+                            in1=mask_pit[:, r0 : r0 + CH, :].unsqueeze(1).to_broadcast([P, DQ, CH, PACK]),
+                            op=ALU.mult,
+                        )
+                    else:
+                        nc.vector.tensor_copy(out=dst, in_=view)
+            if is_a:
+                for q in on_scalar:
+                    flat = g[q][:].rearrange("p d r t -> p d (r t)")
+                    nc.vector.tensor_tensor(
+                        out=flat,
+                        in0=flat,
+                        in1=mask_pit[:, row0 : row0 + ROWS, :]
+                        .rearrange("p r t -> p (r t)")
+                        .unsqueeze(1)
+                        .to_broadcast([P, DQ, ROWS * PACK]),
+                        op=ALU.mult,
+                    )
+                for q in range(NQ):
+                    for dl in range(DQ):
+                        d = q * DQ + dl
+                        nc.vector.quantize_mx(
+                            out=a_codes[:, d, row0 : row0 + ROWS].bitcast(FP8X4),
+                            scales=a_scales[:, d, row0 : row0 + ROWS],
+                            in_=g[q][:, dl, :, :].rearrange("p r t -> p (r t)"),
+                        )
+            else:
+                for q in range(NQ):
+                    for e in range(2):
+                        dl0 = e * (DQ // 2)
+                        d0 = q * DQ + dl0
+                        nc.vector.quantize_mx(
+                            out=b_codes[:, d0 : d0 + DQ // 2, :].rearrange("p d j -> p (d j)").bitcast(FP8X4),
+                            scales=b_scales[:, d0 : d0 + DQ // 2, :].rearrange("p d j -> p (d j)"),
+                            in_=g[q][:, dl0 : dl0 + DQ // 2, :, :].rearrange("p d r t -> p (d r t)"),
+                        )
+
+        t_sb = [grp.tile([P, JH, ND], F32, tag="g", name="t_sb%d" % h, align_bytes=64) for h in range(NJ // JH)]
+        for bank in range(ND // DBANK):
+            acc = psum.tile([P, DBANK, NJ], F32, tag="bank")
+            for dl in range(DBANK):
+                d = bank * DBANK + dl
+                nc.tensor.matmul_mx(
+                    out=acc[:, dl, :],
+                    lhsT=a_codes[:, d, :].bitcast(FP8X4),
+                    lhsT_scale=a_scales[:, d, :],
+                    rhs=b_codes[:, d, :].bitcast(FP8X4),
+                    rhs_scale=b_scales[:, d, :],
+                    start=True,
+                    stop=True,
+                )
+            for h in range(NJ // JH):
+                nc.scalar.copy(
+                    out=t_sb[h][:, :, bank * DBANK : (bank + 1) * DBANK],
+                    in_=acc[:, :, h * JH : (h + 1) * JH].rearrange("p d j -> p j d"),
+                )
+
+        stats = small.tile([P, NJ, 6], F32)
+        for j in range(NJ):
+            nc.vector.bn_stats(out=stats[:, j, :], in_=t_sb[j // JH][:, j % JH, :])
+        mean2 = small.tile([P, NJ], F32)
+        nc.vector.tensor_tensor(out=mean2[:], in0=stats[:, :, 1], in1=stats[:, :, 4], op=ALU.add)
+        diff = small.tile([P, NJ], F32)
+        nc.vector.tensor_tensor(out=diff[:], in0=stats[:, :, 1], in1=stats[:, :, 4], op=ALU.subtract)
+        m2 = small.tile([P, NJ], F32)
+        nc.vector.tensor_tensor(out=m2[:], in0=stats[:, :, 2], in1=stats[:, :, 5], op=ALU.add)
+        diff2 = small.tile([P, NJ], F32)
+        nc.vector.tensor_tensor(out=diff2[:], in0=diff[:], in1=diff[:], op=ALU.mult)
+        var4 = small.tile([P, NJ], F32)
+        nc.vector.scalar_tensor_tensor(
+            out=var4[:], in0=m2[:], scalar=1.0 / 32.0, in1=diff2[:], op0=ALU.mult, op1=ALU.add
+        )
+        std = small.tile([P, NJ], F32)
+        nc.scalar.activation(out=std[:], in_=var4[:], func=ACT.Sqrt, scale=0.25, bias=eps_t[:, 0:1])
+        rstd = small.tile([P, NJ], F32)
+        nc.vector.reciprocal(out=rstd[:], in_=std[:])
+        shift = small.tile([P, NJ], F32)
+        nc.vector.scalar_tensor_tensor(
+            out=shift[:], in0=mean2[:], scalar=-0.5, in1=rstd[:], op0=ALU.mult, op1=ALU.mult
+        )
+
+        for jb in range(NJ // JB):
+            j0 = jb * JB
+            blk = t_sb[j0 // JH][:, j0 % JH : j0 % JH + JB, :]
+            for j in range(j0, j0 + JB):
+                row = t_sb[j // JH][:, j % JH, :]
+                nc.scalar.activation(
+                    out=row, in_=row, func=ACT.Identity, scale=rstd[:, j : j + 1], bias=shift[:, j : j + 1]
+                )
+            nc.vector.tensor_tensor(
+                out=blk, in0=blk, in1=wb[:, 0, :].unsqueeze(1).to_broadcast([P, JB, ND]), op=ALU.mult
+            )
+            nc.vector.tensor_tensor(
+                out=blk, in0=blk, in1=wb[:, 1, :].unsqueeze(1).to_broadcast([P, JB, ND]), op=ALU.add
+            )
+            nc.sync.dma_start(out=out[:, j0 : j0 + JB, :], in_=blk)

@@ -17,17 +17,17 @@ NI, NJ, NK, ND = 128, 64, 512, 128
 EPS = 1e-5
 FLOPS = 2 * NI * NJ * NK * ND
 
-ROWS = 64
 CH = 8
-NCH = ROWS // CH
-DQ = 32
-NQ = ND // DQ
-DBANK = 8
+RB = 4
+IH = 64
+DH = 64
 JH = 32
+DBANK = 8
 JB = 16
+QW = 4096
 
-SCALAR_Q_A = (0, 1, 2)
-SCALAR_Q_B = (0, 1)
+VECTOR_S1_A = (3, 7)
+VECTOR_S1_B = (3,)
 
 
 def tile_trianglemultiplication_pa_kernel(tc, a_gated, b_gated, mask, norm_out_w, norm_out_b, out):
@@ -36,13 +36,14 @@ def tile_trianglemultiplication_pa_kernel(tc, a_gated, b_gated, mask, norm_out_w
         keep = ctx.enter_context(tc.tile_pool(name="keep", bufs=1))
         small = ctx.enter_context(tc.tile_pool(name="small", bufs=1))
         rawp = ctx.enter_context(tc.tile_pool(name="rawp", bufs=3))
-        grp = ctx.enter_context(tc.tile_pool(name="grp", bufs=5))
+        s1p = ctx.enter_context(tc.tile_pool(name="s1p", bufs=2))
+        grp = ctx.enter_context(tc.tile_pool(name="grp", bufs=2))
         psum = ctx.enter_context(tc.psum_pool(name="psum", bufs=8))
 
         a_codes = keep.tile([P, ND, NI], U32, align_bytes=64)
         a_scales = keep.tile([P, ND, NI], U8, align_bytes=64)
-        b_codes = keep.tile([P, ND, NJ], U32, align_bytes=64)
-        b_scales = keep.tile([P, ND, NJ], U8, align_bytes=64)
+        b_codes = [keep.tile([P, ND, JH], U32, name="b_codes%d" % h, align_bytes=64) for h in range(NJ // JH)]
+        b_scales = [keep.tile([P, ND, JH], U8, name="b_scales%d" % h, align_bytes=64) for h in range(NJ // JH)]
 
         eps_t = small.tile([P, 1], F32)
         nc.vector.memset(eps_t[:], EPS)
@@ -67,121 +68,128 @@ def tile_trianglemultiplication_pa_kernel(tc, a_gated, b_gated, mask, norm_out_w
         wb = small.tile([P, 2, ND], F32)
         nc.vector.tensor_copy(out=wb[:], in_=wb16[:])
 
-        groups = ((a_gated, 0, True), (a_gated, ROWS, True), (b_gated, 0, False))
-        for gi, (src, row0, is_a) in enumerate(groups):
-            on_scalar = SCALAR_Q_A if is_a else SCALAR_Q_B
+        def words_of_rows(src, r0, on_vector):
+            raw = rawp.tile([P, CH, PACK, ND], BF16, tag="raw")
+            nc.sync.dma_start(
+                out=raw[:].rearrange("p r t d -> p r (t d)"),
+                in_=src[r0 : r0 + CH].rearrange("r (p t) d -> p r (t d)", t=PACK),
+            )
+            s1 = s1p.tile([P, CH, ND, PACK], BF16, tag="s1")
+            view = raw[:].rearrange("p r t d -> p r d t")
+            if on_vector:
+                nc.vector.tensor_copy(out=s1[:], in_=view)
+            else:
+                nc.scalar.copy(out=s1[:], in_=view)
+            return s1
+
+        for ih in range(NI // IH):
             g = [
-                grp.tile([P, DQ, ROWS, PACK], BF16, tag="g", name="g%d_%d" % (gi, q), align_bytes=64)
-                for q in range(NQ)
+                grp.tile([P, DH, IH, PACK], BF16, tag="g", name="ga%d_%d" % (ih, dh), align_bytes=64)
+                for dh in range(ND // DH)
             ]
-            for c in range(NCH):
-                r0 = row0 + c * CH
-                raw = rawp.tile([P, CH, PACK, ND], BF16, tag="raw")
-                nc.sync.dma_start(
-                    out=raw[:].rearrange("p r t d -> p r (t d)"),
-                    in_=src[r0 : r0 + CH].rearrange("r (p t) d -> p r (t d)", t=PACK),
-                )
-                for q in range(NQ):
-                    dst = g[q][:, :, c * CH : (c + 1) * CH, :]
-                    view = raw[:, :, :, q * DQ : (q + 1) * DQ].rearrange("p r t d -> p d r t")
-                    if q in on_scalar:
-                        nc.scalar.copy(out=dst, in_=view)
-                    elif is_a:
+            for c in range(IH // CH):
+                s1 = words_of_rows(a_gated, ih * IH + c * CH, c in VECTOR_S1_A)
+                for rb in range(CH // RB):
+                    rl = rb * RB
+                    rg = c * CH + rl
+                    i0 = ih * IH + rg
+                    for dh in range(ND // DH):
                         nc.vector.tensor_tensor(
-                            out=dst,
-                            in0=view,
-                            in1=mask_pit[:, r0 : r0 + CH, :].unsqueeze(1).to_broadcast([P, DQ, CH, PACK]),
+                            out=g[dh][:, :, rg : rg + RB, :],
+                            in0=s1[:, rl : rl + RB, dh * DH : (dh + 1) * DH, :].rearrange("p r d t -> p d r t"),
+                            in1=mask_pit[:, i0 : i0 + RB, :].unsqueeze(1).to_broadcast([P, DH, RB, PACK]),
                             op=ALU.mult,
                         )
-                    else:
-                        nc.vector.tensor_copy(out=dst, in_=view)
-            if is_a:
-                for q in on_scalar:
-                    flat = g[q][:].rearrange("p d r t -> p d (r t)")
-                    nc.vector.tensor_tensor(
-                        out=flat,
-                        in0=flat,
-                        in1=mask_pit[:, row0 : row0 + ROWS, :]
-                        .rearrange("p r t -> p (r t)")
-                        .unsqueeze(1)
-                        .to_broadcast([P, DQ, ROWS * PACK]),
-                        op=ALU.mult,
+            for d in range(ND):
+                nc.vector.quantize_mx(
+                    out=a_codes[:, d, ih * IH : (ih + 1) * IH].bitcast(FP8X4),
+                    scales=a_scales[:, d, ih * IH : (ih + 1) * IH],
+                    in_=g[d // DH][:, d % DH, :, :].rearrange("p r t -> p (r t)"),
+                )
+
+        for h in range(NJ // JH):
+            gb = grp.tile([P, ND, JH, PACK], BF16, tag="g", name="gb%d" % h, align_bytes=64)
+            for c in range(JH // CH):
+                s1 = words_of_rows(b_gated, h * JH + c * CH, c in VECTOR_S1_B)
+                for rb in range(CH // RB):
+                    rl = rb * RB
+                    rg = c * CH + rl
+                    nc.vector.tensor_copy(
+                        out=gb[:, :, rg : rg + RB, :],
+                        in_=s1[:, rl : rl + RB, :, :].rearrange("p r d t -> p d r t"),
                     )
-                for q in range(NQ):
-                    for dl in range(DQ):
-                        d = q * DQ + dl
-                        nc.vector.quantize_mx(
-                            out=a_codes[:, d, row0 : row0 + ROWS].bitcast(FP8X4),
-                            scales=a_scales[:, d, row0 : row0 + ROWS],
-                            in_=g[q][:, dl, :, :].rearrange("p r t -> p (r t)"),
-                        )
-            else:
-                for q in range(NQ):
-                    for e in range(2):
-                        dl0 = e * (DQ // 2)
-                        d0 = q * DQ + dl0
-                        nc.vector.quantize_mx(
-                            out=b_codes[:, d0 : d0 + DQ // 2, :].rearrange("p d j -> p (d j)").bitcast(FP8X4),
-                            scales=b_scales[:, d0 : d0 + DQ // 2, :].rearrange("p d j -> p (d j)"),
-                            in_=g[q][:, dl0 : dl0 + DQ // 2, :, :].rearrange("p d r t -> p (d r t)"),
-                        )
-
-        t_sb = [grp.tile([P, JH, ND], F32, tag="g", name="t_sb%d" % h, align_bytes=64) for h in range(NJ // JH)]
-        for bank in range(ND // DBANK):
-            acc = psum.tile([P, DBANK, NJ], F32, tag="bank")
-            for dl in range(DBANK):
-                d = bank * DBANK + dl
-                nc.tensor.matmul_mx(
-                    out=acc[:, dl, :],
-                    lhsT=a_codes[:, d, :].bitcast(FP8X4),
-                    lhsT_scale=a_scales[:, d, :],
-                    rhs=b_codes[:, d, :].bitcast(FP8X4),
-                    rhs_scale=b_scales[:, d, :],
-                    start=True,
-                    stop=True,
+            dq = QW // (JH * PACK)
+            for d0 in range(0, ND, dq):
+                nc.vector.quantize_mx(
+                    out=b_codes[h][:, d0 : d0 + dq, :].rearrange("p d j -> p (d j)").bitcast(FP8X4),
+                    scales=b_scales[h][:, d0 : d0 + dq, :].rearrange("p d j -> p (d j)"),
+                    in_=gb[:, d0 : d0 + dq, :, :].rearrange("p d r t -> p (d r t)"),
                 )
-            for h in range(NJ // JH):
+
+        t_sb = []
+        for h in range(NJ // JH):
+            t_h = grp.tile([P, JH, ND], F32, tag="g", name="t_sb%d" % h, align_bytes=64)
+            t_sb.append(t_h)
+            for bank in range(ND // DBANK):
+                acc = psum.tile([P, DBANK * 2 * JH], F32, tag="bank")
+                for s in range(DBANK):
+                    d = bank * DBANK + s
+                    d2 = d - d % 2
+                    nc.tensor.matmul_mx(
+                        out=acc[:, s * 2 * JH : (s + 1) * 2 * JH],
+                        lhsT=a_codes[:, d, :].bitcast(FP8X4),
+                        lhsT_scale=a_scales[:, d, :],
+                        rhs=b_codes[h][:, d2 : d2 + 2, :].rearrange("p d j -> p (d j)").bitcast(FP8X4),
+                        rhs_scale=b_scales[h][:, d2 : d2 + 2, :].rearrange("p d j -> p (d j)"),
+                        start=True,
+                        stop=True,
+                    )
                 nc.scalar.copy(
-                    out=t_sb[h][:, :, bank * DBANK : (bank + 1) * DBANK],
-                    in_=acc[:, :, h * JH : (h + 1) * JH].rearrange("p d j -> p j d"),
+                    out=t_h[:, :, bank * DBANK : (bank + 1) * DBANK].rearrange("p j (dp e) -> p j dp e", e=2),
+                    in_=acc[:]
+                    .rearrange("p (dp c j) -> p dp c j", c=4, j=JH)[:, :, 0:4:3, :]
+                    .rearrange("p dp e j -> p j dp e"),
                 )
 
-        stats = small.tile([P, NJ, 6], F32)
-        for j in range(NJ):
-            nc.vector.bn_stats(out=stats[:, j, :], in_=t_sb[j // JH][:, j % JH, :])
-        mean2 = small.tile([P, NJ], F32)
-        nc.vector.tensor_tensor(out=mean2[:], in0=stats[:, :, 1], in1=stats[:, :, 4], op=ALU.add)
-        diff = small.tile([P, NJ], F32)
-        nc.vector.tensor_tensor(out=diff[:], in0=stats[:, :, 1], in1=stats[:, :, 4], op=ALU.subtract)
-        m2 = small.tile([P, NJ], F32)
-        nc.vector.tensor_tensor(out=m2[:], in0=stats[:, :, 2], in1=stats[:, :, 5], op=ALU.add)
-        diff2 = small.tile([P, NJ], F32)
-        nc.vector.tensor_tensor(out=diff2[:], in0=diff[:], in1=diff[:], op=ALU.mult)
-        var4 = small.tile([P, NJ], F32)
-        nc.vector.scalar_tensor_tensor(
-            out=var4[:], in0=m2[:], scalar=1.0 / 32.0, in1=diff2[:], op0=ALU.mult, op1=ALU.add
-        )
-        std = small.tile([P, NJ], F32)
-        nc.scalar.activation(out=std[:], in_=var4[:], func=ACT.Sqrt, scale=0.25, bias=eps_t[:, 0:1])
-        rstd = small.tile([P, NJ], F32)
-        nc.vector.reciprocal(out=rstd[:], in_=std[:])
-        shift = small.tile([P, NJ], F32)
-        nc.vector.scalar_tensor_tensor(
-            out=shift[:], in0=mean2[:], scalar=-0.5, in1=rstd[:], op0=ALU.mult, op1=ALU.mult
-        )
-
-        for jb in range(NJ // JB):
-            j0 = jb * JB
-            blk = t_sb[j0 // JH][:, j0 % JH : j0 % JH + JB, :]
-            for j in range(j0, j0 + JB):
-                row = t_sb[j // JH][:, j % JH, :]
-                nc.scalar.activation(
-                    out=row, in_=row, func=ACT.Identity, scale=rstd[:, j : j + 1], bias=shift[:, j : j + 1]
+        for h in range(NJ // JH):
+            t_h = t_sb[h]
+            stats = small.tile([P, JH, 6], F32, name="stats%d" % h)
+            for j in range(JH):
+                nc.vector.bn_stats(out=stats[:, j, :], in_=t_h[:, j, :])
+            mean2 = small.tile([P, JH], F32, name="mean2_%d" % h)
+            nc.vector.tensor_tensor(out=mean2[:], in0=stats[:, :, 1], in1=stats[:, :, 4], op=ALU.add)
+            diff = small.tile([P, JH], F32, name="diff%d" % h)
+            nc.vector.tensor_tensor(out=diff[:], in0=stats[:, :, 1], in1=stats[:, :, 4], op=ALU.subtract)
+            m2 = small.tile([P, JH], F32, name="m2_%d" % h)
+            nc.vector.tensor_tensor(out=m2[:], in0=stats[:, :, 2], in1=stats[:, :, 5], op=ALU.add)
+            diff2 = small.tile([P, JH], F32, name="diff2_%d" % h)
+            nc.vector.tensor_tensor(out=diff2[:], in0=diff[:], in1=diff[:], op=ALU.mult)
+            var4 = small.tile([P, JH], F32, name="var4_%d" % h)
+            nc.vector.scalar_tensor_tensor(
+                out=var4[:], in0=m2[:], scalar=1.0 / 32.0, in1=diff2[:], op0=ALU.mult, op1=ALU.add
+            )
+            std = small.tile([P, JH], F32, name="std%d" % h)
+            nc.scalar.activation(out=std[:], in_=var4[:], func=ACT.Sqrt, scale=0.25, bias=eps_t[:, 0:1])
+            rstd = small.tile([P, JH], F32, name="rstd%d" % h)
+            nc.vector.reciprocal(out=rstd[:], in_=std[:])
+            shift = small.tile([P, JH], F32, name="shift%d" % h)
+            nc.vector.scalar_tensor_tensor(
+                out=shift[:], in0=mean2[:], scalar=-0.5, in1=rstd[:], op0=ALU.mult, op1=ALU.mult
+            )
+            for j0 in range(0, JH, JB):
+                blk = t_h[:, j0 : j0 + JB, :]
+                for j in range(j0, j0 + JB):
+                    nc.scalar.activation(
+                        out=t_h[:, j, :],
+                        in_=t_h[:, j, :],
+                        func=ACT.Identity,
+                        scale=rstd[:, j : j + 1],
+                        bias=shift[:, j : j + 1],
+                    )
+                nc.vector.tensor_tensor(
+                    out=blk, in0=blk, in1=wb[:, 0, :].unsqueeze(1).to_broadcast([P, JB, ND]), op=ALU.mult
                 )
-            nc.vector.tensor_tensor(
-                out=blk, in0=blk, in1=wb[:, 0, :].unsqueeze(1).to_broadcast([P, JB, ND]), op=ALU.mult
-            )
-            nc.vector.tensor_tensor(
-                out=blk, in0=blk, in1=wb[:, 1, :].unsqueeze(1).to_broadcast([P, JB, ND]), op=ALU.add
-            )
-            nc.sync.dma_start(out=out[:, j0 : j0 + JB, :], in_=blk)
+                nc.vector.tensor_tensor(
+                    out=blk, in0=blk, in1=wb[:, 1, :].unsqueeze(1).to_broadcast([P, JB, ND]), op=ALU.add
+                )
+                nc.sync.dma_start(out=out[:, h * JH + j0 : h * JH + j0 + JB, :], in_=blk)

@@ -17,7 +17,7 @@ NI, NJ, NK, ND = 128, 64, 512, 128
 EPS = 1e-5
 FLOPS = 2 * NI * NJ * NK * ND
 
-CH = 8
+CH = 4
 RB = 4
 IH = 64
 DH = 64
@@ -26,8 +26,8 @@ DBANK = 8
 JB = 16
 QW = 4096
 
-VECTOR_S1_A = (3, 7)
-VECTOR_S1_B = (3,)
+VECTOR_S1_A = ((0, 1, 3, 5, 8, 11, 13), (9, 13, 15))
+VECTOR_S1_B = ((7,), (4, 6, 7))
 
 
 def tile_trianglemultiplication_pa_kernel(tc, a_gated, b_gated, mask, norm_out_w, norm_out_b, out):
@@ -35,10 +35,11 @@ def tile_trianglemultiplication_pa_kernel(tc, a_gated, b_gated, mask, norm_out_w
     with ExitStack() as ctx:
         keep = ctx.enter_context(tc.tile_pool(name="keep", bufs=1))
         small = ctx.enter_context(tc.tile_pool(name="small", bufs=1))
-        rawp = ctx.enter_context(tc.tile_pool(name="rawp", bufs=3))
-        s1p = ctx.enter_context(tc.tile_pool(name="s1p", bufs=2))
+        rawp = ctx.enter_context(tc.tile_pool(name="rawp", bufs=4))
+        s1p = ctx.enter_context(tc.tile_pool(name="s1p", bufs=6))
         grp = ctx.enter_context(tc.tile_pool(name="grp", bufs=2))
         psum = ctx.enter_context(tc.psum_pool(name="psum", bufs=8))
+        ctx.enter_context(tc.manual_schedule())
 
         a_codes = keep.tile([P, ND, NI], U32, align_bytes=64)
         a_scales = keep.tile([P, ND, NI], U8, align_bytes=64)
@@ -65,8 +66,6 @@ def tile_trianglemultiplication_pa_kernel(tc, a_gated, b_gated, mask, norm_out_w
         wb16 = small.tile([P, 2, ND], BF16)
         nc.scalar.dma_start(out=wb16[:, 0, :], in_=norm_out_w.partition_broadcast(P))
         nc.scalar.dma_start(out=wb16[:, 1, :], in_=norm_out_b.partition_broadcast(P))
-        wb = small.tile([P, 2, ND], F32)
-        nc.vector.tensor_copy(out=wb[:], in_=wb16[:])
 
         def words_of_rows(src, r0, on_vector):
             raw = rawp.tile([P, CH, PACK, ND], BF16, tag="raw")
@@ -88,7 +87,7 @@ def tile_trianglemultiplication_pa_kernel(tc, a_gated, b_gated, mask, norm_out_w
                 for dh in range(ND // DH)
             ]
             for c in range(IH // CH):
-                s1 = words_of_rows(a_gated, ih * IH + c * CH, c in VECTOR_S1_A)
+                s1 = words_of_rows(a_gated, ih * IH + c * CH, c in VECTOR_S1_A[ih])
                 for rb in range(CH // RB):
                     rl = rb * RB
                     rg = c * CH + rl
@@ -110,7 +109,7 @@ def tile_trianglemultiplication_pa_kernel(tc, a_gated, b_gated, mask, norm_out_w
         for h in range(NJ // JH):
             gb = grp.tile([P, ND, JH, PACK], BF16, tag="g", name="gb%d" % h, align_bytes=64)
             for c in range(JH // CH):
-                s1 = words_of_rows(b_gated, h * JH + c * CH, c in VECTOR_S1_B)
+                s1 = words_of_rows(b_gated, h * JH + c * CH, c in VECTOR_S1_B[h])
                 for rb in range(CH // RB):
                     rl = rb * RB
                     rg = c * CH + rl
@@ -151,7 +150,12 @@ def tile_trianglemultiplication_pa_kernel(tc, a_gated, b_gated, mask, norm_out_w
                     .rearrange("p dp e j -> p j dp e"),
                 )
 
-        for h in range(NJ // JH):
+        wb = small.tile([P, 2, ND], F32)
+        nc.vector.tensor_copy(out=wb[:], in_=wb16[:])
+        rstd = [small.tile([P, JH], F32, name="rstd%d" % h) for h in range(NJ // JH)]
+        shift = [small.tile([P, JH], F32, name="shift%d" % h) for h in range(NJ // JH)]
+
+        def statistics(h):
             t_h = t_sb[h]
             stats = small.tile([P, JH, 6], F32, name="stats%d" % h)
             for j in range(JH):
@@ -170,22 +174,24 @@ def tile_trianglemultiplication_pa_kernel(tc, a_gated, b_gated, mask, norm_out_w
             )
             std = small.tile([P, JH], F32, name="std%d" % h)
             nc.scalar.activation(out=std[:], in_=var4[:], func=ACT.Sqrt, scale=0.25, bias=eps_t[:, 0:1])
-            rstd = small.tile([P, JH], F32, name="rstd%d" % h)
-            nc.vector.reciprocal(out=rstd[:], in_=std[:])
-            shift = small.tile([P, JH], F32, name="shift%d" % h)
+            nc.vector.reciprocal(out=rstd[h][:], in_=std[:])
             nc.vector.scalar_tensor_tensor(
-                out=shift[:], in0=mean2[:], scalar=-0.5, in1=rstd[:], op0=ALU.mult, op1=ALU.mult
+                out=shift[h][:], in0=mean2[:], scalar=-0.5, in1=rstd[h][:], op0=ALU.mult, op1=ALU.mult
             )
+
+        def normalise(h):
+            for j in range(JH):
+                nc.scalar.activation(
+                    out=t_sb[h][:, j, :],
+                    in_=t_sb[h][:, j, :],
+                    func=ACT.Identity,
+                    scale=rstd[h][:, j : j + 1],
+                    bias=shift[h][:, j : j + 1],
+                )
+
+        def gain_bias_store(h):
             for j0 in range(0, JH, JB):
-                blk = t_h[:, j0 : j0 + JB, :]
-                for j in range(j0, j0 + JB):
-                    nc.scalar.activation(
-                        out=t_h[:, j, :],
-                        in_=t_h[:, j, :],
-                        func=ACT.Identity,
-                        scale=rstd[:, j : j + 1],
-                        bias=shift[:, j : j + 1],
-                    )
+                blk = t_sb[h][:, j0 : j0 + JB, :]
                 nc.vector.tensor_tensor(
                     out=blk, in0=blk, in1=wb[:, 0, :].unsqueeze(1).to_broadcast([P, JB, ND]), op=ALU.mult
                 )
@@ -193,3 +199,10 @@ def tile_trianglemultiplication_pa_kernel(tc, a_gated, b_gated, mask, norm_out_w
                     out=blk, in0=blk, in1=wb[:, 1, :].unsqueeze(1).to_broadcast([P, JB, ND]), op=ALU.add
                 )
                 nc.sync.dma_start(out=out[:, h * JH + j0 : h * JH + j0 + JB, :], in_=blk)
+
+        statistics(0)
+        normalise(0)
+        statistics(1)
+        gain_bias_store(0)
+        normalise(1)
+        gain_bias_store(1)

@@ -20,14 +20,13 @@ FLOPS = 2 * NI * NJ * NK * ND
 CH = 4
 RB = 4
 IH = 64
-DH = 64
 JH = 32
-DBANK = 8
-JB = 16
+DBANK = 4
 QW = 4096
 
-VECTOR_S1_A = ((0, 1, 3, 5, 8, 11, 13), (9, 13, 15))
-VECTOR_S1_B = ((7,), (4, 6, 7))
+VECTOR_S1_A = ((0, 1, 3, 6, 8, 11, 13, 15), (9, 11, 13, 15))
+VECTOR_S1_B = ((7,), (3, 4, 6, 7))
+STORE_J = (16, 8)
 
 
 def tile_trianglemultiplication_pa_kernel(tc, a_gated, b_gated, mask, norm_out_w, norm_out_b, out):
@@ -37,7 +36,7 @@ def tile_trianglemultiplication_pa_kernel(tc, a_gated, b_gated, mask, norm_out_w
         small = ctx.enter_context(tc.tile_pool(name="small", bufs=1))
         rawp = ctx.enter_context(tc.tile_pool(name="rawp", bufs=4))
         s1p = ctx.enter_context(tc.tile_pool(name="s1p", bufs=6))
-        grp = ctx.enter_context(tc.tile_pool(name="grp", bufs=2))
+        grp = ctx.enter_context(tc.tile_pool(name="grp", bufs=1))
         psum = ctx.enter_context(tc.psum_pool(name="psum", bufs=8))
         ctx.enter_context(tc.manual_schedule())
 
@@ -46,6 +45,9 @@ def tile_trianglemultiplication_pa_kernel(tc, a_gated, b_gated, mask, norm_out_w
         b_codes = [keep.tile([P, ND, JH], U32, name="b_codes%d" % h, align_bytes=64) for h in range(NJ // JH)]
         b_scales = [keep.tile([P, ND, JH], U8, name="b_scales%d" % h, align_bytes=64) for h in range(NJ // JH)]
 
+        mask_ik = small.tile([P, NK], BF16)
+        nc.scalar.dma_start(out=mask_ik[:], in_=mask)
+
         eps_t = small.tile([P, 1], F32)
         nc.vector.memset(eps_t[:], EPS)
         warm = small.tile([P, 1], F32)
@@ -53,8 +55,6 @@ def tile_trianglemultiplication_pa_kernel(tc, a_gated, b_gated, mask, norm_out_w
 
         ident = small.tile([P, P], BF16)
         make_identity(nc, ident[:])
-        mask_ik = small.tile([P, NK], BF16)
-        nc.sync.dma_start(out=mask_ik[:], in_=mask)
         mask_itp = small.tile([P, PACK, P], BF16)
         nc.vector.tensor_copy(out=mask_itp[:], in_=mask_ik[:].rearrange("i (p t) -> i t p", t=PACK))
         mask_ps = psum.tile([P, PACK, P], BF16, tag="bank")
@@ -76,38 +76,34 @@ def tile_trianglemultiplication_pa_kernel(tc, a_gated, b_gated, mask, norm_out_w
             s1 = s1p.tile([P, CH, ND, PACK], BF16, tag="s1")
             view = raw[:].rearrange("p r t d -> p r d t")
             if on_vector:
-                nc.vector.tensor_copy(out=s1[:], in_=view)
+                nc.vector.tensor_copy(
+                    out=s1[:].rearrange("p r (c i) t -> p r c t i", i=4),
+                    in_=raw[:].rearrange("p r t (c i) -> p r c t i", i=4),
+                )
             else:
                 nc.scalar.copy(out=s1[:], in_=view)
             return s1
 
         for ih in range(NI // IH):
-            g = [
-                grp.tile([P, DH, IH, PACK], BF16, tag="g", name="ga%d_%d" % (ih, dh), align_bytes=64)
-                for dh in range(ND // DH)
-            ]
+            ga = grp.tile([P, ND, IH, PACK], BF16, name="ga%d" % ih, offset=0, align_bytes=64)
             for c in range(IH // CH):
                 s1 = words_of_rows(a_gated, ih * IH + c * CH, c in VECTOR_S1_A[ih])
-                for rb in range(CH // RB):
-                    rl = rb * RB
-                    rg = c * CH + rl
-                    i0 = ih * IH + rg
-                    for dh in range(ND // DH):
-                        nc.vector.tensor_tensor(
-                            out=g[dh][:, :, rg : rg + RB, :],
-                            in0=s1[:, rl : rl + RB, dh * DH : (dh + 1) * DH, :].rearrange("p r d t -> p d r t"),
-                            in1=mask_pit[:, i0 : i0 + RB, :].unsqueeze(1).to_broadcast([P, DH, RB, PACK]),
-                            op=ALU.mult,
-                        )
+                i0 = ih * IH + c * CH
+                nc.vector.tensor_tensor(
+                    out=ga[:, :, c * CH : (c + 1) * CH, :],
+                    in0=s1[:].rearrange("p r d t -> p d r t"),
+                    in1=mask_pit[:, i0 : i0 + CH, :].unsqueeze(1).to_broadcast([P, ND, CH, PACK]),
+                    op=ALU.mult,
+                )
             for d in range(ND):
                 nc.vector.quantize_mx(
                     out=a_codes[:, d, ih * IH : (ih + 1) * IH].bitcast(FP8X4),
                     scales=a_scales[:, d, ih * IH : (ih + 1) * IH],
-                    in_=g[d // DH][:, d % DH, :, :].rearrange("p r t -> p (r t)"),
+                    in_=ga[:, d, :, :].rearrange("p r t -> p (r t)"),
                 )
 
         for h in range(NJ // JH):
-            gb = grp.tile([P, ND, JH, PACK], BF16, tag="g", name="gb%d" % h, align_bytes=64)
+            gb = grp.tile([P, ND, JH, PACK], BF16, name="gb%d" % h, offset=h * ND * JH * PACK * 2, align_bytes=64)
             for c in range(JH // CH):
                 s1 = words_of_rows(b_gated, h * JH + c * CH, c in VECTOR_S1_B[h])
                 for rb in range(CH // RB):
@@ -127,27 +123,26 @@ def tile_trianglemultiplication_pa_kernel(tc, a_gated, b_gated, mask, norm_out_w
 
         t_sb = []
         for h in range(NJ // JH):
-            t_h = grp.tile([P, JH, ND], F32, tag="g", name="t_sb%d" % h, align_bytes=64)
+            t_h = grp.tile([P, JH, ND], F32, name="t_sb%d" % h, offset=h * JH * ND * 4, align_bytes=64)
             t_sb.append(t_h)
             for bank in range(ND // DBANK):
-                acc = psum.tile([P, DBANK * 2 * JH], F32, tag="bank")
+                d0 = bank * DBANK
+                acc = psum.tile([P, DBANK * DBANK * JH], F32, tag="bank")
                 for s in range(DBANK):
-                    d = bank * DBANK + s
-                    d2 = d - d % 2
                     nc.tensor.matmul_mx(
-                        out=acc[:, s * 2 * JH : (s + 1) * 2 * JH],
-                        lhsT=a_codes[:, d, :].bitcast(FP8X4),
-                        lhsT_scale=a_scales[:, d, :],
-                        rhs=b_codes[h][:, d2 : d2 + 2, :].rearrange("p d j -> p (d j)").bitcast(FP8X4),
-                        rhs_scale=b_scales[h][:, d2 : d2 + 2, :].rearrange("p d j -> p (d j)"),
+                        out=acc[:, s * DBANK * JH : (s + 1) * DBANK * JH],
+                        lhsT=a_codes[:, d0 + s, :].bitcast(FP8X4),
+                        lhsT_scale=a_scales[:, d0 + s, :],
+                        rhs=b_codes[h][:, d0 : d0 + DBANK, :].rearrange("p d j -> p (d j)").bitcast(FP8X4),
+                        rhs_scale=b_scales[h][:, d0 : d0 + DBANK, :].rearrange("p d j -> p (d j)"),
                         start=True,
                         stop=True,
                     )
                 nc.scalar.copy(
-                    out=t_h[:, :, bank * DBANK : (bank + 1) * DBANK].rearrange("p j (dp e) -> p j dp e", e=2),
+                    out=t_h[:, :, d0 : d0 + DBANK],
                     in_=acc[:]
-                    .rearrange("p (dp c j) -> p dp c j", c=4, j=JH)[:, :, 0:4:3, :]
-                    .rearrange("p dp e j -> p j dp e"),
+                    .rearrange("p (c j) -> p c j", j=JH)[:, 0 : DBANK * DBANK : DBANK + 1, :]
+                    .rearrange("p s j -> p j s"),
                 )
 
         wb = small.tile([P, 2, ND], F32)
@@ -190,15 +185,16 @@ def tile_trianglemultiplication_pa_kernel(tc, a_gated, b_gated, mask, norm_out_w
                 )
 
         def gain_bias_store(h):
-            for j0 in range(0, JH, JB):
-                blk = t_sb[h][:, j0 : j0 + JB, :]
+            jb = STORE_J[h]
+            for j0 in range(0, JH, jb):
+                blk = t_sb[h][:, j0 : j0 + jb, :]
                 nc.vector.tensor_tensor(
-                    out=blk, in0=blk, in1=wb[:, 0, :].unsqueeze(1).to_broadcast([P, JB, ND]), op=ALU.mult
+                    out=blk, in0=blk, in1=wb[:, 0, :].unsqueeze(1).to_broadcast([P, jb, ND]), op=ALU.mult
                 )
                 nc.vector.tensor_tensor(
-                    out=blk, in0=blk, in1=wb[:, 1, :].unsqueeze(1).to_broadcast([P, JB, ND]), op=ALU.add
+                    out=blk, in0=blk, in1=wb[:, 1, :].unsqueeze(1).to_broadcast([P, jb, ND]), op=ALU.add
                 )
-                nc.sync.dma_start(out=out[:, h * JH + j0 : h * JH + j0 + JB, :], in_=blk)
+                nc.sync.dma_start(out=out[:, h * JH + j0 : h * JH + j0 + jb, :], in_=blk)
 
         statistics(0)
         normalise(0)

@@ -24,9 +24,11 @@ JH = 32
 DBANK = 4
 QW = 4096
 
-VECTOR_S1_A = ((0, 1, 3, 6, 8, 11, 13, 15), (9, 11, 13, 15))
-VECTOR_S1_B = ((7,), (3, 4, 6, 7))
+VECTOR_S1_A = ((0, 1, 3, 5, 8, 10, 13), (8, 10, 12))
+VECTOR_S1_B = ((7,), (0, 4, 6, 7))
 STORE_J = (16, 8)
+ROOT0_AFTER_BANK = 25
+ROOT1_AFTER_J = 16
 
 
 def tile_trianglemultiplication_pa_kernel(tc, a_gated, b_gated, mask, norm_out_w, norm_out_b, out):
@@ -34,7 +36,7 @@ def tile_trianglemultiplication_pa_kernel(tc, a_gated, b_gated, mask, norm_out_w
     with ExitStack() as ctx:
         keep = ctx.enter_context(tc.tile_pool(name="keep", bufs=1))
         small = ctx.enter_context(tc.tile_pool(name="small", bufs=1))
-        rawp = ctx.enter_context(tc.tile_pool(name="rawp", bufs=4))
+        rawp = ctx.enter_context(tc.tile_pool(name="rawp", bufs=6))
         s1p = ctx.enter_context(tc.tile_pool(name="s1p", bufs=6))
         grp = ctx.enter_context(tc.tile_pool(name="grp", bufs=1))
         psum = ctx.enter_context(tc.psum_pool(name="psum", bufs=8))
@@ -45,7 +47,7 @@ def tile_trianglemultiplication_pa_kernel(tc, a_gated, b_gated, mask, norm_out_w
         b_codes = [keep.tile([P, ND, JH], U32, name="b_codes%d" % h, align_bytes=64) for h in range(NJ // JH)]
         b_scales = [keep.tile([P, ND, JH], U8, name="b_scales%d" % h, align_bytes=64) for h in range(NJ // JH)]
 
-        mask_ik = small.tile([P, NK], BF16)
+        mask_ik = grp.tile([P, NK], BF16, offset=0, align_bytes=64)
         nc.scalar.dma_start(out=mask_ik[:], in_=mask)
 
         eps_t = small.tile([P, 1], F32)
@@ -55,7 +57,7 @@ def tile_trianglemultiplication_pa_kernel(tc, a_gated, b_gated, mask, norm_out_w
 
         ident = small.tile([P, P], BF16)
         make_identity(nc, ident[:])
-        mask_itp = small.tile([P, PACK, P], BF16)
+        mask_itp = grp.tile([P, PACK, P], BF16, offset=NK * 2, align_bytes=64)
         nc.vector.tensor_copy(out=mask_itp[:], in_=mask_ik[:].rearrange("i (p t) -> i t p", t=PACK))
         mask_ps = psum.tile([P, PACK, P], BF16, tag="bank")
         for t in range(PACK):
@@ -121,11 +123,13 @@ def tile_trianglemultiplication_pa_kernel(tc, a_gated, b_gated, mask, norm_out_w
                     in_=gb[:, d0 : d0 + dq, :, :].rearrange("p d r t -> p (d r t)"),
                 )
 
-        t_sb = []
-        for h in range(NJ // JH):
-            t_h = grp.tile([P, JH, ND], F32, name="t_sb%d" % h, offset=h * JH * ND * 4, align_bytes=64)
-            t_sb.append(t_h)
-            for bank in range(ND // DBANK):
+        t_sb = [
+            grp.tile([P, JH, ND], F32, name="t_sb%d" % h, offset=h * JH * ND * 4, align_bytes=64)
+            for h in range(NJ // JH)
+        ]
+
+        def products(h, banks):
+            for bank in banks:
                 d0 = bank * DBANK
                 acc = psum.tile([P, DBANK * DBANK * JH], F32, tag="bank")
                 for s in range(DBANK):
@@ -139,43 +143,55 @@ def tile_trianglemultiplication_pa_kernel(tc, a_gated, b_gated, mask, norm_out_w
                         stop=True,
                     )
                 nc.scalar.copy(
-                    out=t_h[:, :, d0 : d0 + DBANK],
+                    out=t_sb[h][:, :, d0 : d0 + DBANK],
                     in_=acc[:]
                     .rearrange("p (c j) -> p c j", j=JH)[:, 0 : DBANK * DBANK : DBANK + 1, :]
                     .rearrange("p s j -> p j s"),
                 )
 
-        wb = small.tile([P, 2, ND], F32)
-        nc.vector.tensor_copy(out=wb[:], in_=wb16[:])
-        rstd = [small.tile([P, JH], F32, name="rstd%d" % h) for h in range(NJ // JH)]
-        shift = [small.tile([P, JH], F32, name="shift%d" % h) for h in range(NJ // JH)]
+        late_offset = [ND * JH * PACK * 2]
 
-        def statistics(h):
-            t_h = t_sb[h]
-            stats = small.tile([P, JH, 6], F32, name="stats%d" % h)
+        def late_tile(shape, name):
+            size = 4
+            for n in shape[1:]:
+                size *= n
+            t = grp.tile(shape, F32, name=name, offset=late_offset[0], align_bytes=64)
+            late_offset[0] += (size + 63) // 64 * 64
+            return t
+
+        wb = late_tile([P, 2, ND], "wb")
+        stats = [late_tile([P, JH, 6], "stats%d" % h) for h in range(NJ // JH)]
+        mean2 = [late_tile([P, JH], "mean2_%d" % h) for h in range(NJ // JH)]
+        diff = [late_tile([P, JH], "diff%d" % h) for h in range(NJ // JH)]
+        m2 = [late_tile([P, JH], "m2_%d" % h) for h in range(NJ // JH)]
+        var4 = [late_tile([P, JH], "var4_%d" % h) for h in range(NJ // JH)]
+        std = [late_tile([P, JH], "std%d" % h) for h in range(NJ // JH)]
+        rstd = [late_tile([P, JH], "rstd%d" % h) for h in range(NJ // JH)]
+        shift = [late_tile([P, JH], "shift%d" % h) for h in range(NJ // JH)]
+
+        def moments(h):
             for j in range(JH):
-                nc.vector.bn_stats(out=stats[:, j, :], in_=t_h[:, j, :])
-            mean2 = small.tile([P, JH], F32, name="mean2_%d" % h)
-            nc.vector.tensor_tensor(out=mean2[:], in0=stats[:, :, 1], in1=stats[:, :, 4], op=ALU.add)
-            diff = small.tile([P, JH], F32, name="diff%d" % h)
-            nc.vector.tensor_tensor(out=diff[:], in0=stats[:, :, 1], in1=stats[:, :, 4], op=ALU.subtract)
-            m2 = small.tile([P, JH], F32, name="m2_%d" % h)
-            nc.vector.tensor_tensor(out=m2[:], in0=stats[:, :, 2], in1=stats[:, :, 5], op=ALU.add)
-            diff2 = small.tile([P, JH], F32, name="diff2_%d" % h)
-            nc.vector.tensor_tensor(out=diff2[:], in0=diff[:], in1=diff[:], op=ALU.mult)
-            var4 = small.tile([P, JH], F32, name="var4_%d" % h)
+                nc.vector.bn_stats(out=stats[h][:, j, :], in_=t_sb[h][:, j, :])
+            st = stats[h]
+            nc.vector.tensor_tensor(out=mean2[h][:], in0=st[:, :, 1], in1=st[:, :, 4], op=ALU.add)
+            nc.vector.tensor_tensor(out=diff[h][:], in0=st[:, :, 1], in1=st[:, :, 4], op=ALU.subtract)
+            nc.vector.tensor_tensor(out=m2[h][:], in0=st[:, :, 2], in1=st[:, :, 5], op=ALU.add)
+            nc.vector.tensor_tensor(out=diff[h][:], in0=diff[h][:], in1=diff[h][:], op=ALU.mult)
             nc.vector.scalar_tensor_tensor(
-                out=var4[:], in0=m2[:], scalar=1.0 / 32.0, in1=diff2[:], op0=ALU.mult, op1=ALU.add
-            )
-            std = small.tile([P, JH], F32, name="std%d" % h)
-            nc.scalar.activation(out=std[:], in_=var4[:], func=ACT.Sqrt, scale=0.25, bias=eps_t[:, 0:1])
-            nc.vector.reciprocal(out=rstd[h][:], in_=std[:])
-            nc.vector.scalar_tensor_tensor(
-                out=shift[h][:], in0=mean2[:], scalar=-0.5, in1=rstd[h][:], op0=ALU.mult, op1=ALU.mult
+                out=var4[h][:], in0=m2[h][:], scalar=1.0 / 32.0, in1=diff[h][:], op0=ALU.mult, op1=ALU.add
             )
 
-        def normalise(h):
-            for j in range(JH):
+        def root(h):
+            nc.scalar.activation(out=std[h][:], in_=var4[h][:], func=ACT.Sqrt, scale=0.25, bias=eps_t[:, 0:1])
+
+        def scale_and_shift(h):
+            nc.vector.reciprocal(out=rstd[h][:], in_=std[h][:])
+            nc.vector.scalar_tensor_tensor(
+                out=shift[h][:], in0=mean2[h][:], scalar=-0.5, in1=rstd[h][:], op0=ALU.mult, op1=ALU.mult
+            )
+
+        def normalise(h, js):
+            for j in js:
                 nc.scalar.activation(
                     out=t_sb[h][:, j, :],
                     in_=t_sb[h][:, j, :],
@@ -196,9 +212,19 @@ def tile_trianglemultiplication_pa_kernel(tc, a_gated, b_gated, mask, norm_out_w
                 )
                 nc.sync.dma_start(out=out[:, h * JH + j0 : h * JH + j0 + jb, :], in_=blk)
 
-        statistics(0)
-        normalise(0)
-        statistics(1)
+        n_banks = ND // DBANK
+        products(0, range(n_banks))
+        nc.vector.tensor_copy(out=wb[:], in_=wb16[:])
+        moments(0)
+        products(1, range(ROOT0_AFTER_BANK))
+        root(0)
+        products(1, range(ROOT0_AFTER_BANK, n_banks))
+        scale_and_shift(0)
+        normalise(0, range(ROOT1_AFTER_J))
+        moments(1)
+        root(1)
+        scale_and_shift(1)
+        normalise(0, range(ROOT1_AFTER_J, JH))
         gain_bias_store(0)
-        normalise(1)
+        normalise(1, range(JH))
         gain_bias_store(1)

@@ -76,14 +76,17 @@ def tile_trianglemultiplication_pa_kernel(tc, a_gated, b_gated, mask, norm_out_w
                 in_=src[r0 : r0 + CH].rearrange("r (p t) d -> p r (t d)", t=PACK),
             )
             s1 = s1p.tile([P, CH, ND, PACK], BF16, tag="s1")
-            view = raw[:].rearrange("p r t d -> p r d t")
             if on_vector:
                 nc.vector.tensor_copy(
                     out=s1[:].rearrange("p r (c i) t -> p r c t i", i=4),
                     in_=raw[:].rearrange("p r t (c i) -> p r c t i", i=4),
                 )
             else:
-                nc.scalar.copy(out=s1[:], in_=view)
+                for r in range(CH):
+                    nc.scalar.copy(
+                        out=s1[:, r, :, :].rearrange("p (c i) t -> p c t i", i=4),
+                        in_=raw[:, r, :, :].rearrange("p t (c i) -> p c t i", i=4),
+                    )
             return s1
 
         for ih in range(NI // IH):

@@ -24,8 +24,8 @@ JH = 32
 DBANK = 4
 QW = 4096
 
-VECTOR_S1_A = ((0, 1, 3, 5, 8, 10, 13), (8, 10, 12))
-VECTOR_S1_B = ((7,), (0, 4, 6, 7))
+VECTOR_S1_A = ((0, 1, 3, 5, 9, 11), (10, 14))
+VECTOR_S1_B = ((7,), (3, 5, 7))
 STORE_J = (16, 8)
 ROOT0_AFTER_BANK = 25
 ROOT1_AFTER_J = 16

@@ -40,7 +40,6 @@ def tile_trianglemultiplication_pa_kernel(tc, a_gated, b_gated, mask, norm_out_w
         s1p = ctx.enter_context(tc.tile_pool(name="s1p", bufs=6))
         grp = ctx.enter_context(tc.tile_pool(name="grp", bufs=1))
         psum = ctx.enter_context(tc.psum_pool(name="psum", bufs=8))
-        ctx.enter_context(tc.manual_schedule())
 
         a_codes = keep.tile([P, ND, NI], U32, align_bytes=64)
         a_scales = keep.tile([P, ND, NI], U8, align_bytes=64)

@@ -23,6 +23,12 @@ IH = 64
 JH = 32
 DBANK = 4
 QW = 4096
+SLOT_BYTES = CH * PACK * ND * 2
+SLOTS_B = 12
+RAW_SLOTS_B = tuple(range(0, 6))
+S1_SLOTS_B = tuple(range(6, 12))
+RAW_SLOTS_A = tuple(range(0, 10))
+S1_SLOTS_A = tuple(range(10, 22))
 
 VECTOR_S1_A = ((0, 1, 3, 5, 9, 11), (10, 14))
 VECTOR_S1_B = ((7,), (3, 5, 7))
@@ -36,15 +42,22 @@ def tile_trianglemultiplication_pa_kernel(tc, a_gated, b_gated, mask, norm_out_w
     with ExitStack() as ctx:
         keep = ctx.enter_context(tc.tile_pool(name="keep", bufs=1))
         small = ctx.enter_context(tc.tile_pool(name="small", bufs=1))
-        rawp = ctx.enter_context(tc.tile_pool(name="rawp", bufs=6))
-        s1p = ctx.enter_context(tc.tile_pool(name="s1p", bufs=6))
+        ring = ctx.enter_context(tc.tile_pool(name="ring", bufs=1))
         grp = ctx.enter_context(tc.tile_pool(name="grp", bufs=1))
         psum = ctx.enter_context(tc.psum_pool(name="psum", bufs=8))
 
         a_codes = keep.tile([P, ND, NI], U32, align_bytes=64)
         a_scales = keep.tile([P, ND, NI], U8, align_bytes=64)
-        b_codes = [keep.tile([P, ND, JH], U32, name="b_codes%d" % h, align_bytes=64) for h in range(NJ // JH)]
-        b_scales = [keep.tile([P, ND, JH], U8, name="b_scales%d" % h, align_bytes=64) for h in range(NJ // JH)]
+        b_base = SLOTS_B * SLOT_BYTES
+        b_codes = [
+            ring.tile([P, ND, JH], U32, name="b_codes%d" % h, offset=b_base + h * ND * JH * 4, align_bytes=64)
+            for h in range(NJ // JH)
+        ]
+        b_scales = [
+            ring.tile([P, ND, JH], U8, name="b_scales%d" % h, offset=b_base + NJ * ND * 4 + h * ND * JH, align_bytes=64)
+            for h in range(NJ // JH)
+        ]
+        n_loads = [0]
 
         mask_ik = grp.tile([P, NK], BF16, offset=0, align_bytes=64)
         nc.scalar.dma_start(out=mask_ik[:], in_=mask)
@@ -68,13 +81,19 @@ def tile_trianglemultiplication_pa_kernel(tc, a_gated, b_gated, mask, norm_out_w
         nc.scalar.dma_start(out=wb16[:, 0, :], in_=norm_out_w.partition_broadcast(P))
         nc.scalar.dma_start(out=wb16[:, 1, :], in_=norm_out_b.partition_broadcast(P))
 
-        def words_of_rows(src, r0, on_vector):
-            raw = rawp.tile([P, CH, PACK, ND], BF16, tag="raw")
+        def words_of_rows(src, r0, on_vector, raw_slots, s1_slots):
+            n = n_loads[0]
+            n_loads[0] += 1
+            raw = ring.tile(
+                [P, CH, PACK, ND], BF16, name="raw%d" % n, offset=raw_slots[n % len(raw_slots)] * SLOT_BYTES, align_bytes=64
+            )
             nc.sync.dma_start(
                 out=raw[:].rearrange("p r t d -> p r (t d)"),
                 in_=src[r0 : r0 + CH].rearrange("r (p t) d -> p r (t d)", t=PACK),
             )
-            s1 = s1p.tile([P, CH, ND, PACK], BF16, tag="s1")
+            s1 = ring.tile(
+                [P, CH, ND, PACK], BF16, name="s1_%d" % n, offset=s1_slots[n % len(s1_slots)] * SLOT_BYTES, align_bytes=64
+            )
             if on_vector:
                 nc.vector.tensor_copy(
                     out=s1[:].rearrange("p r (c i) t -> p r c t i", i=4),
@@ -91,7 +110,7 @@ def tile_trianglemultiplication_pa_kernel(tc, a_gated, b_gated, mask, norm_out_w
         for ih in range(NI // IH):
             ga = grp.tile([P, ND, IH, PACK], BF16, name="ga%d" % ih, offset=0, align_bytes=64)
             for c in range(IH // CH):
-                s1 = words_of_rows(a_gated, ih * IH + c * CH, c in VECTOR_S1_A[ih])
+                s1 = words_of_rows(a_gated, ih * IH + c * CH, c in VECTOR_S1_A[ih], RAW_SLOTS_A, S1_SLOTS_A)
                 i0 = ih * IH + c * CH
                 nc.vector.tensor_tensor(
                     out=ga[:, :, c * CH : (c + 1) * CH, :],
@@ -109,7 +128,7 @@ def tile_trianglemultiplication_pa_kernel(tc, a_gated, b_gated, mask, norm_out_w
         for h in range(NJ // JH):
             gb = grp.tile([P, ND, JH, PACK], BF16, name="gb%d" % h, offset=h * ND * JH * PACK * 2, align_bytes=64)
             for c in range(JH // CH):
-                s1 = words_of_rows(b_gated, h * JH + c * CH, c in VECTOR_S1_B[h])
+                s1 = words_of_rows(b_gated, h * JH + c * CH, c in VECTOR_S1_B[h], RAW_SLOTS_B, S1_SLOTS_B)
                 for rb in range(CH // RB):
                     rl = rb * RB
                     rg = c * CH + rl

@@ -34,7 +34,6 @@ VECTOR_S1_A = ((0, 1, 3, 5, 9, 11), (10, 14))
 VECTOR_S1_B = ((7,), (3, 5, 7))
 STORE_J = (16, 8)
 ROOT0_AFTER_BANK = 25
-ROOT1_AFTER_J = 16
 
 
 def tile_trianglemultiplication_pa_kernel(tc, a_gated, b_gated, mask, norm_out_w, norm_out_b, out):
@@ -221,9 +220,20 @@ def tile_trianglemultiplication_pa_kernel(tc, a_gated, b_gated, mask, norm_out_w
                     bias=shift[h][:, j : j + 1],
                 )
 
-        def gain_bias_store(h):
+        def normalise_on_vector(h, js):
+            for j in js:
+                nc.vector.tensor_scalar(
+                    out=t_sb[h][:, j, :],
+                    in0=t_sb[h][:, j, :],
+                    scalar1=rstd[h][:, j : j + 1],
+                    scalar2=shift[h][:, j : j + 1],
+                    op0=ALU.mult,
+                    op1=ALU.add,
+                )
+
+        def gain_bias_store(h, blocks):
             jb = STORE_J[h]
-            for j0 in range(0, JH, jb):
+            for j0 in blocks:
                 blk = t_sb[h][:, j0 : j0 + jb, :]
                 nc.vector.tensor_tensor(
                     out=blk, in0=blk, in1=wb[:, 0, :].unsqueeze(1).to_broadcast([P, jb, ND]), op=ALU.mult
@@ -241,11 +251,12 @@ def tile_trianglemultiplication_pa_kernel(tc, a_gated, b_gated, mask, norm_out_w
         root(0)
         products(1, range(ROOT0_AFTER_BANK, n_banks))
         scale_and_shift(0)
-        normalise(0, range(ROOT1_AFTER_J))
+        normalise_on_vector(0, range(STORE_J[0]))
+        gain_bias_store(0, (0,))
+        normalise(0, range(STORE_J[0], JH))
         moments(1)
         root(1)
         scale_and_shift(1)
-        normalise(0, range(ROOT1_AFTER_J, JH))
-        gain_bias_store(0)
+        gain_bias_store(0, (STORE_J[0],))
         normalise(1, range(JH))
-        gain_bias_store(1)
+        gain_bias_store(1, range(0, JH, STORE_J[1]))

@@ -32,7 +32,9 @@ S1_SLOTS_A = tuple(range(10, 22))
 
 VECTOR_S1_A = ((0, 1, 3, 5, 9, 11), (10, 14))
 VECTOR_S1_B = ((7,), (3, 5, 7))
-STORE_J = (16, 8)
+JG = 4
+SCALED_BUFS = 4
+VECTOR_FROM_GROUP = 4
 ROOT0_AFTER_BANK = 25
 
 
@@ -79,6 +81,13 @@ def tile_trianglemultiplication_pa_kernel(tc, a_gated, b_gated, mask, norm_out_w
         wb16 = small.tile([P, 2, ND], BF16)
         nc.scalar.dma_start(out=wb16[:, 0, :], in_=norm_out_w.partition_broadcast(P))
         nc.scalar.dma_start(out=wb16[:, 1, :], in_=norm_out_b.partition_broadcast(P))
+        wb_ps = psum.tile([P, 2, P], BF16, tag="bank")
+        for n in range(2):
+            nc.tensor.transpose(wb_ps[:, n, :], wb16[:, n, :], ident[:])
+        wb_col = small.tile([P, 2], F32)
+        nc.vector.tensor_copy(out=wb_col[:], in_=wb_ps[:, :, 0])
+        ident_f32 = small.tile([P, P], F32)
+        make_identity(nc, ident_f32[:])
 
         def words_of_rows(src, r0, on_vector, raw_slots, s1_slots):
             n = n_loads[0]
@@ -179,7 +188,6 @@ def tile_trianglemultiplication_pa_kernel(tc, a_gated, b_gated, mask, norm_out_w
             late_offset[0] += (size + 63) // 64 * 64
             return t
 
-        wb = late_tile([P, 2, ND], "wb")
         stats = [late_tile([P, JH, 6], "stats%d" % h) for h in range(NJ // JH)]
         mean2 = [late_tile([P, JH], "mean2_%d" % h) for h in range(NJ // JH)]
         diff = [late_tile([P, JH], "diff%d" % h) for h in range(NJ // JH)]
@@ -231,32 +239,68 @@ def tile_trianglemultiplication_pa_kernel(tc, a_gated, b_gated, mask, norm_out_w
                     op1=ALU.add,
                 )
 
-        def gain_bias_store(h, blocks):
-            jb = STORE_J[h]
-            for j0 in blocks:
-                blk = t_sb[h][:, j0 : j0 + jb, :]
-                nc.vector.tensor_tensor(
-                    out=blk, in0=blk, in1=wb[:, 0, :].unsqueeze(1).to_broadcast([P, jb, ND]), op=ALU.mult
-                )
-                nc.vector.tensor_tensor(
-                    out=blk, in0=blk, in1=wb[:, 1, :].unsqueeze(1).to_broadcast([P, jb, ND]), op=ALU.add
-                )
-                nc.sync.dma_start(out=out[:, h * JH + j0 : h * JH + j0 + jb, :], in_=blk)
+        turned = {}
+        scaled = {}
+        back = {}
+        n_scaled = [0]
+
+        def turn(h, g):
+            bank = psum.tile([P, JG, P], F32, tag="bank")
+            for n in range(JG):
+                nc.tensor.transpose(bank[:, n, :], t_sb[h][:, g * JG + n, :], ident_f32[:])
+            turned[h, g] = bank
+
+        def gain_bias(h, g):
+            n = n_scaled[0]
+            n_scaled[0] += 1
+            tile = ring.tile([P, JG, P], F32, name="scaled%d" % n, offset=(n % SCALED_BUFS) * JG * P * 4, align_bytes=64)
+            nc.scalar.activation(
+                out=tile[:], in_=turned[h, g][:], func=ACT.Identity, scale=wb_col[:, 0:1], bias=wb_col[:, 1:2]
+            )
+            scaled[h, g] = tile
+
+        def turn_back(h, g):
+            bank = psum.tile([P, JG, P], F32, tag="bank")
+            for n in range(JG):
+                nc.tensor.transpose(bank[:, n, :], scaled[h, g][:, n, :], ident_f32[:])
+            back[h, g] = bank
+
+        def out_of_psum_and_store(h, g):
+            nc.vector.tensor_copy(out=t_sb[h][:, g * JG : (g + 1) * JG, :], in_=back[h, g][:])
+            if g % 2 == 1:
+                j0 = (g - 1) * JG
+                nc.sync.dma_start(out=out[:, h * JH + j0 : h * JH + j0 + 2 * JG, :], in_=t_sb[h][:, j0 : j0 + 2 * JG, :])
 
         n_banks = ND // DBANK
+        n_groups = JH // JG
         products(0, range(n_banks))
-        nc.vector.tensor_copy(out=wb[:], in_=wb16[:])
         moments(0)
         products(1, range(ROOT0_AFTER_BANK))
         root(0)
         products(1, range(ROOT0_AFTER_BANK, n_banks))
         scale_and_shift(0)
-        normalise_on_vector(0, range(STORE_J[0]))
-        gain_bias_store(0, (0,))
-        normalise(0, range(STORE_J[0], JH))
+        normalise_on_vector(0, range(JH))
+        for g in range(n_groups):
+            turn(0, g)
         moments(1)
+        for g in range(n_groups):
+            gain_bias(0, g)
+            turn_back(0, g)
         root(1)
+        out_of_psum_and_store(0, 0)
+        out_of_psum_and_store(0, 1)
         scale_and_shift(1)
-        gain_bias_store(0, (STORE_J[0],))
-        normalise(1, range(JH))
-        gain_bias_store(1, range(0, JH, STORE_J[1]))
+        for g in range(2, n_groups):
+            out_of_psum_and_store(0, g)
+        normalise_on_vector(1, range(VECTOR_FROM_GROUP * JG, JH))
+        for s in range(n_groups + 4):
+            if s < VECTOR_FROM_GROUP:
+                normalise(1, range(s * JG, (s + 1) * JG))
+            if 0 <= s - 1 < n_groups:
+                turn(1, s - 1)
+            if 0 <= s - 2 < n_groups:
+                gain_bias(1, s - 2)
+            if 0 <= s - 3 < n_groups:
+                turn_back(1, s - 3)
+            if 0 <= s - 4 < n_groups:
+                out_of_psum_and_store(1, s - 4)

@@ -23,6 +23,7 @@ IH = 64
 JH = 32
 DBANK = 4
 QW = 4096
+RUN = 8
 SLOT_BYTES = CH * PACK * ND * 2
 SLOTS_B = 12
 RAW_SLOTS_B = tuple(range(0, 6))
@@ -104,14 +105,14 @@ def tile_trianglemultiplication_pa_kernel(tc, a_gated, b_gated, mask, norm_out_w
             )
             if on_vector:
                 nc.vector.tensor_copy(
-                    out=s1[:].rearrange("p r (c i) t -> p r c t i", i=4),
-                    in_=raw[:].rearrange("p r t (c i) -> p r c t i", i=4),
+                    out=s1[:].rearrange("p r (c i) t -> p r c t i", i=RUN),
+                    in_=raw[:].rearrange("p r t (c i) -> p r c t i", i=RUN),
                 )
             else:
                 for r in range(CH):
                     nc.scalar.copy(
-                        out=s1[:, r, :, :].rearrange("p (c i) t -> p c t i", i=4),
-                        in_=raw[:, r, :, :].rearrange("p t (c i) -> p c t i", i=4),
+                        out=s1[:, r, :, :].rearrange("p (c i) t -> p c t i", i=RUN),
+                        in_=raw[:, r, :, :].rearrange("p t (c i) -> p c t i", i=RUN),
                     )
             return s1
 
@@ -197,25 +198,29 @@ def tile_trianglemultiplication_pa_kernel(tc, a_gated, b_gated, mask, norm_out_w
         rstd = [late_tile([P, JH], "rstd%d" % h) for h in range(NJ // JH)]
         shift = [late_tile([P, JH], "shift%d" % h) for h in range(NJ // JH)]
 
-        def moments(h):
-            for j in range(JH):
+        def moments(h, j0=0, j1=JH):
+            for j in range(j0, j1):
                 nc.vector.bn_stats(out=stats[h][:, j, :], in_=t_sb[h][:, j, :])
-            st = stats[h]
-            nc.vector.tensor_tensor(out=mean2[h][:], in0=st[:, :, 1], in1=st[:, :, 4], op=ALU.add)
-            nc.vector.tensor_tensor(out=diff[h][:], in0=st[:, :, 1], in1=st[:, :, 4], op=ALU.subtract)
-            nc.vector.tensor_tensor(out=m2[h][:], in0=st[:, :, 2], in1=st[:, :, 5], op=ALU.add)
-            nc.vector.tensor_tensor(out=diff[h][:], in0=diff[h][:], in1=diff[h][:], op=ALU.mult)
+            st = stats[h][:, j0:j1, :]
+            js = slice(j0, j1)
+            nc.vector.tensor_tensor(out=mean2[h][:, js], in0=st[:, :, 1], in1=st[:, :, 4], op=ALU.add)
+            nc.vector.tensor_tensor(out=diff[h][:, js], in0=st[:, :, 1], in1=st[:, :, 4], op=ALU.subtract)
+            nc.vector.tensor_tensor(out=m2[h][:, js], in0=st[:, :, 2], in1=st[:, :, 5], op=ALU.add)
+            nc.vector.tensor_tensor(out=diff[h][:, js], in0=diff[h][:, js], in1=diff[h][:, js], op=ALU.mult)
             nc.vector.scalar_tensor_tensor(
-                out=var4[h][:], in0=m2[h][:], scalar=1.0 / 32.0, in1=diff[h][:], op0=ALU.mult, op1=ALU.add
+                out=var4[h][:, js], in0=m2[h][:, js], scalar=1.0 / 32.0, in1=diff[h][:, js], op0=ALU.mult, op1=ALU.add
             )
 
-        def root(h):
-            nc.scalar.activation(out=std[h][:], in_=var4[h][:], func=ACT.Sqrt, scale=0.25, bias=eps_t[:, 0:1])
+        def root(h, j0=0, j1=JH):
+            nc.scalar.activation(
+                out=std[h][:, j0:j1], in_=var4[h][:, j0:j1], func=ACT.Sqrt, scale=0.25, bias=eps_t[:, 0:1]
+            )
 
-        def scale_and_shift(h):
-            nc.vector.reciprocal(out=rstd[h][:], in_=std[h][:])
+        def scale_and_shift(h, j0=0, j1=JH):
+            js = slice(j0, j1)
+            nc.vector.reciprocal(out=rstd[h][:, js], in_=std[h][:, js])
             nc.vector.scalar_tensor_tensor(
-                out=shift[h][:], in0=mean2[h][:], scalar=-0.5, in1=rstd[h][:], op0=ALU.mult, op1=ALU.mult
+                out=shift[h][:, js], in0=mean2[h][:, js], scalar=-0.5, in1=rstd[h][:, js], op0=ALU.mult, op1=ALU.mult
             )
 
         def normalise(h, js):
@@ -282,14 +287,21 @@ def tile_trianglemultiplication_pa_kernel(tc, a_gated, b_gated, mask, norm_out_w
         normalise_on_vector(0, range(JH))
         for g in range(n_groups):
             turn(0, g)
-        moments(1)
-        for g in range(n_groups):
+        half = JH // 2
+        moments(1, 0, half)
+        for g in range(n_groups // 2):
             gain_bias(0, g)
             turn_back(0, g)
-        root(1)
+        root(1, 0, half)
+        moments(1, half, JH)
+        scale_and_shift(1, 0, half)
+        for g in range(n_groups // 2, n_groups):
+            gain_bias(0, g)
+            turn_back(0, g)
+        root(1, half, JH)
         out_of_psum_and_store(0, 0)
         out_of_psum_and_store(0, 1)
-        scale_and_shift(1)
+        scale_and_shift(1, half, JH)
         for g in range(2, n_groups):
             out_of_psum_and_store(0, g)
         normalise_on_vector(1, range(VECTOR_FROM_GROUP * JG, JH))

@@ -18,21 +18,21 @@ EPS = 1e-5
 FLOPS = 2 * NI * NJ * NK * ND
 
 CH = 4
-RB = 4
 IH = 64
 JH = 32
 DBANK = 4
 QW = 4096
-RUN = 8
+RUN = 4
 SLOT_BYTES = CH * PACK * ND * 2
-SLOTS_B = 12
-RAW_SLOTS_B = tuple(range(0, 6))
-S1_SLOTS_B = tuple(range(6, 12))
+CODE_SLOT = 12
 RAW_SLOTS_A = tuple(range(0, 10))
 S1_SLOTS_A = tuple(range(10, 22))
+GB0_SLOT = 0
+RAW_SLOTS_B0 = (8, 9, 18, 19, 20, 21, 10, 11)
+RAW_SLOTS_B1 = (8, 9, 10, 11)
 
 VECTOR_S1_A = ((0, 1, 3, 5, 9, 11), (10, 14))
-VECTOR_S1_B = ((7,), (3, 5, 7))
+VECTOR_S1_B = ((6, 7), (1, 3, 5, 7))
 JG = 4
 SCALED_BUFS = 4
 VECTOR_FROM_GROUP = 4
@@ -50,7 +50,7 @@ def tile_trianglemultiplication_pa_kernel(tc, a_gated, b_gated, mask, norm_out_w
 
         a_codes = keep.tile([P, ND, NI], U32, align_bytes=64)
         a_scales = keep.tile([P, ND, NI], U8, align_bytes=64)
-        b_base = SLOTS_B * SLOT_BYTES
+        b_base = CODE_SLOT * SLOT_BYTES
         b_codes = [
             ring.tile([P, ND, JH], U32, name="b_codes%d" % h, offset=b_base + h * ND * JH * 4, align_bytes=64)
             for h in range(NJ // JH)
@@ -59,8 +59,6 @@ def tile_trianglemultiplication_pa_kernel(tc, a_gated, b_gated, mask, norm_out_w
             ring.tile([P, ND, JH], U8, name="b_scales%d" % h, offset=b_base + NJ * ND * 4 + h * ND * JH, align_bytes=64)
             for h in range(NJ // JH)
         ]
-        n_loads = [0]
-
         mask_ik = grp.tile([P, NK], BF16, offset=0, align_bytes=64)
         nc.scalar.dma_start(out=mask_ik[:], in_=mask)
 
@@ -90,40 +88,38 @@ def tile_trianglemultiplication_pa_kernel(tc, a_gated, b_gated, mask, norm_out_w
         ident_f32 = small.tile([P, P], F32)
         make_identity(nc, ident_f32[:])
 
-        def words_of_rows(src, r0, on_vector, raw_slots, s1_slots):
-            n = n_loads[0]
-            n_loads[0] += 1
-            raw = ring.tile(
-                [P, CH, PACK, ND], BF16, name="raw%d" % n, offset=raw_slots[n % len(raw_slots)] * SLOT_BYTES, align_bytes=64
-            )
+        def load(src, r0, pool, offset, name):
+            raw = pool.tile([P, CH, PACK, ND], BF16, name=name, offset=offset, align_bytes=64)
             nc.sync.dma_start(
                 out=raw[:].rearrange("p r t d -> p r (t d)"),
                 in_=src[r0 : r0 + CH].rearrange("r (p t) d -> p r (t d)", t=PACK),
             )
-            s1 = ring.tile(
-                [P, CH, ND, PACK], BF16, name="s1_%d" % n, offset=s1_slots[n % len(s1_slots)] * SLOT_BYTES, align_bytes=64
+            return raw
+
+        def regroup(dst, raw, on_vector):
+            copy = nc.vector.tensor_copy if on_vector else nc.scalar.copy
+            copy(
+                out=dst.rearrange("p (c i) r t -> p c (r t) i", i=RUN),
+                in_=raw[:].rearrange("p r t (c i) -> p c (r t) i", i=RUN),
             )
-            if on_vector:
-                nc.vector.tensor_copy(
-                    out=s1[:].rearrange("p r (c i) t -> p r c t i", i=RUN),
-                    in_=raw[:].rearrange("p r t (c i) -> p r c t i", i=RUN),
-                )
-            else:
-                for r in range(CH):
-                    nc.scalar.copy(
-                        out=s1[:, r, :, :].rearrange("p (c i) t -> p c t i", i=RUN),
-                        in_=raw[:, r, :, :].rearrange("p t (c i) -> p c t i", i=RUN),
-                    )
-            return s1
 
         for ih in range(NI // IH):
             ga = grp.tile([P, ND, IH, PACK], BF16, name="ga%d" % ih, offset=0, align_bytes=64)
             for c in range(IH // CH):
-                s1 = words_of_rows(a_gated, ih * IH + c * CH, c in VECTOR_S1_A[ih], RAW_SLOTS_A, S1_SLOTS_A)
-                i0 = ih * IH + c * CH
+                n = ih * (IH // CH) + c
+                i0 = n * CH
+                raw = load(a_gated, i0, ring, RAW_SLOTS_A[n % len(RAW_SLOTS_A)] * SLOT_BYTES, "raw_a%d" % n)
+                s1 = ring.tile(
+                    [P, ND, CH, PACK],
+                    BF16,
+                    name="s1_%d" % n,
+                    offset=S1_SLOTS_A[n % len(S1_SLOTS_A)] * SLOT_BYTES,
+                    align_bytes=64,
+                )
+                regroup(s1[:], raw, c in VECTOR_S1_A[ih])
                 nc.vector.tensor_tensor(
                     out=ga[:, :, c * CH : (c + 1) * CH, :],
-                    in0=s1[:].rearrange("p r d t -> p d r t"),
+                    in0=s1[:],
                     in1=mask_pit[:, i0 : i0 + CH, :].unsqueeze(1).to_broadcast([P, ND, CH, PACK]),
                     op=ALU.mult,
                 )
@@ -135,16 +131,19 @@ def tile_trianglemultiplication_pa_kernel(tc, a_gated, b_gated, mask, norm_out_w
                 )
 
         for h in range(NJ // JH):
-            gb = grp.tile([P, ND, JH, PACK], BF16, name="gb%d" % h, offset=h * ND * JH * PACK * 2, align_bytes=64)
+            if h == 0:
+                gb = ring.tile([P, ND, JH, PACK], BF16, name="gb0", offset=GB0_SLOT * SLOT_BYTES, align_bytes=64)
+            else:
+                gb = grp.tile([P, ND, JH, PACK], BF16, name="gb1", offset=0, align_bytes=64)
             for c in range(JH // CH):
-                s1 = words_of_rows(b_gated, h * JH + c * CH, c in VECTOR_S1_B[h], RAW_SLOTS_B, S1_SLOTS_B)
-                for rb in range(CH // RB):
-                    rl = rb * RB
-                    rg = c * CH + rl
-                    nc.vector.tensor_copy(
-                        out=gb[:, :, rg : rg + RB, :],
-                        in_=s1[:, rl : rl + RB, :, :].rearrange("p r d t -> p d r t"),
-                    )
+                if h == 0:
+                    pool, offset = ring, RAW_SLOTS_B0[c] * SLOT_BYTES
+                elif c < len(RAW_SLOTS_B1):
+                    pool, offset = ring, RAW_SLOTS_B1[c] * SLOT_BYTES
+                else:
+                    pool, offset = grp, ND * JH * PACK * 2 + (c - len(RAW_SLOTS_B1)) * SLOT_BYTES
+                raw = load(b_gated, h * JH + c * CH, pool, offset, "raw_b%d_%d" % (h, c))
+                regroup(gb[:, :, c * CH : (c + 1) * CH, :], raw, c in VECTOR_S1_B[h])
             dq = QW // (JH * PACK)
             for d0 in range(0, ND, dq):
                 nc.vector.quantize_mx(
@@ -153,10 +152,9 @@ def tile_trianglemultiplication_pa_kernel(tc, a_gated, b_gated, mask, norm_out_w
                     in_=gb[:, d0 : d0 + dq, :, :].rearrange("p d r t -> p (d r t)"),
                 )
 
-        t_sb = [
-            grp.tile([P, JH, ND], F32, name="t_sb%d" % h, offset=h * JH * ND * 4, align_bytes=64)
-            for h in range(NJ // JH)
-        ]
+        t_sb0 = grp.tile([P, JH, ND], F32, name="t_sb0", offset=12 * SLOT_BYTES, align_bytes=64)
+        t_sb1 = ring.tile([P, JH, ND], F32, name="t_sb1", offset=GB0_SLOT * SLOT_BYTES, align_bytes=64)
+        t_sb = [t_sb0, t_sb1]
 
         def products(h, banks):
             for bank in banks:
@@ -179,13 +177,13 @@ def tile_trianglemultiplication_pa_kernel(tc, a_gated, b_gated, mask, norm_out_w
                     .rearrange("p s j -> p j s"),
                 )
 
-        late_offset = [ND * JH * PACK * 2]
+        late_offset = [(GB0_SLOT + 6) * SLOT_BYTES]
 
         def late_tile(shape, name):
             size = 4
             for n in shape[1:]:
                 size *= n
-            t = grp.tile(shape, F32, name=name, offset=late_offset[0], align_bytes=64)
+            t = ring.tile(shape, F32, name=name, offset=late_offset[0], align_bytes=64)
             late_offset[0] += (size + 63) // 64 * 64
             return t
 
@@ -258,7 +256,7 @@ def tile_trianglemultiplication_pa_kernel(tc, a_gated, b_gated, mask, norm_out_w
         def gain_bias(h, g):
             n = n_scaled[0]
             n_scaled[0] += 1
-            tile = ring.tile([P, JG, P], F32, name="scaled%d" % n, offset=(n % SCALED_BUFS) * JG * P * 4, align_bytes=64)
+            tile = ring.tile([P, JG, P], F32, name="scaled%d" % n, offset=4 * SLOT_BYTES + (n % SCALED_BUFS) * JG * P * 4, align_bytes=64)
             nc.scalar.activation(
                 out=tile[:], in_=turned[h, g][:], func=ACT.Identity, scale=wb_col[:, 0:1], bias=wb_col[:, 1:2]
             )

@@ -22,7 +22,8 @@ IH = 64
 JH = 32
 DBANK = 4
 QW = 4096
-RUN = 4
+RUN_S = 2
+RUN_V = 4
 SLOT_BYTES = CH * PACK * ND * 2
 CODE_SLOT = 12
 RAW_SLOTS_A = tuple(range(0, 10))
@@ -97,11 +98,16 @@ def tile_trianglemultiplication_pa_kernel(tc, a_gated, b_gated, mask, norm_out_w
             return raw
 
         def regroup(dst, raw, on_vector):
-            copy = nc.vector.tensor_copy if on_vector else nc.scalar.copy
-            copy(
-                out=dst.rearrange("p (c i) r t -> p c (r t) i", i=RUN),
-                in_=raw[:].rearrange("p r t (c i) -> p c (r t) i", i=RUN),
-            )
+            if on_vector:
+                nc.vector.tensor_copy(
+                    out=dst.rearrange("p (c i) r (u e) -> p c (r u) i e", i=RUN_V, e=2),
+                    in_=raw[:].rearrange("p r (u e) (c i) -> p c (r u) i e", i=RUN_V, e=2),
+                )
+            else:
+                nc.scalar.copy(
+                    out=dst.rearrange("p (c i) r t -> p c (r t) i", i=RUN_S),
+                    in_=raw[:].rearrange("p r t (c i) -> p c (r t) i", i=RUN_S),
+                )
 
         for ih in range(NI // IH):
             ga = grp.tile([P, ND, IH, PACK], BF16, name="ga%d" % ih, offset=0, align_bytes=64)

@@ -23,6 +23,7 @@ JH = 32
 DBANK = 4
 QW = 4096
 RUN_S = 2
+RUN_ROW = 8
 RUN_V = 4
 SLOT_BYTES = CH * PACK * ND * 2
 CODE_SLOT = 12
@@ -115,17 +116,27 @@ def tile_trianglemultiplication_pa_kernel(tc, a_gated, b_gated, mask, norm_out_w
                 n = ih * (IH // CH) + c
                 i0 = n * CH
                 raw = load(a_gated, i0, ring, RAW_SLOTS_A[n % len(RAW_SLOTS_A)] * SLOT_BYTES, "raw_a%d" % n)
+                s1_shape = [P, ND, CH, PACK] if c in VECTOR_S1_A[ih] else [P, CH, ND, PACK]
                 s1 = ring.tile(
-                    [P, ND, CH, PACK],
+                    s1_shape,
                     BF16,
                     name="s1_%d" % n,
                     offset=S1_SLOTS_A[n % len(S1_SLOTS_A)] * SLOT_BYTES,
                     align_bytes=64,
                 )
-                regroup(s1[:], raw, c in VECTOR_S1_A[ih])
+                if c in VECTOR_S1_A[ih]:
+                    regroup(s1[:], raw, True)
+                    in0 = s1[:]
+                else:
+                    for r in range(CH):
+                        nc.scalar.copy(
+                            out=s1[:, r, :, :].rearrange("p (c i) t -> p c t i", i=RUN_ROW),
+                            in_=raw[:, r, :, :].rearrange("p t (c i) -> p c t i", i=RUN_ROW),
+                        )
+                    in0 = s1[:].rearrange("p r d t -> p d r t")
                 nc.vector.tensor_tensor(
                     out=ga[:, :, c * CH : (c + 1) * CH, :],
-                    in0=s1[:],
+                    in0=in0,
                     in1=mask_pit[:, i0 : i0 + CH, :].unsqueeze(1).to_broadcast([P, ND, CH, PACK]),
                     op=ALU.mult,
                 )

@@ -22,9 +22,8 @@ IH = 64
 JH = 32
 DBANK = 4
 QW = 4096
-RUN_S = 2
-RUN_ROW = 8
-RUN_V = 4
+RUN = 8
+NG = ND // 4
 SLOT_BYTES = CH * PACK * ND * 2
 CODE_SLOT = 12
 RAW_SLOTS_A = tuple(range(0, 10))
@@ -54,11 +53,13 @@ def tile_trianglemultiplication_pa_kernel(tc, a_gated, b_gated, mask, norm_out_w
         a_scales = keep.tile([P, ND, NI], U8, align_bytes=64)
         b_base = CODE_SLOT * SLOT_BYTES
         b_codes = [
-            ring.tile([P, ND, JH], U32, name="b_codes%d" % h, offset=b_base + h * ND * JH * 4, align_bytes=64)
+            ring.tile([P, NG, JH * DBANK], U32, name="b_codes%d" % h, offset=b_base + h * ND * JH * 4, align_bytes=64)
             for h in range(NJ // JH)
         ]
         b_scales = [
-            ring.tile([P, ND, JH], U8, name="b_scales%d" % h, offset=b_base + NJ * ND * 4 + h * ND * JH, align_bytes=64)
+            ring.tile(
+                [P, NG, JH * DBANK], U8, name="b_scales%d" % h, offset=b_base + NJ * ND * 4 + h * ND * JH, align_bytes=64
+            )
             for h in range(NJ // JH)
         ]
         mask_ik = grp.tile([P, NK], BF16, offset=0, align_bytes=64)
@@ -82,13 +83,23 @@ def tile_trianglemultiplication_pa_kernel(tc, a_gated, b_gated, mask, norm_out_w
         wb16 = small.tile([P, 2, ND], BF16)
         nc.scalar.dma_start(out=wb16[:, 0, :], in_=norm_out_w.partition_broadcast(P))
         nc.scalar.dma_start(out=wb16[:, 1, :], in_=norm_out_b.partition_broadcast(P))
+        wb16_placed = small.tile([P, 2, ND], BF16)
+        nc.vector.tensor_copy(
+            out=wb16_placed[:].rearrange("p n (q g) -> p n q g", q=DBANK),
+            in_=wb16[:].rearrange("p n (g q) -> p n q g", q=DBANK),
+        )
         wb_ps = psum.tile([P, 2, P], BF16, tag="bank")
         for n in range(2):
-            nc.tensor.transpose(wb_ps[:, n, :], wb16[:, n, :], ident[:])
+            nc.tensor.transpose(wb_ps[:, n, :], wb16_placed[:, n, :], ident[:])
         wb_col = small.tile([P, 2], F32)
         nc.vector.tensor_copy(out=wb_col[:], in_=wb_ps[:, :, 0])
         ident_f32 = small.tile([P, P], F32)
         make_identity(nc, ident_f32[:])
+        unplace = small.tile([P, P], F32)
+        nc.vector.tensor_copy(
+            out=unplace[:].rearrange("p (g q) -> p q g", q=DBANK),
+            in_=ident_f32[:].rearrange("p (q g) -> p q g", q=DBANK),
+        )
 
         def load(src, r0, pool, offset, name):
             raw = pool.tile([P, CH, PACK, ND], BF16, name=name, offset=offset, align_bytes=64)
@@ -98,17 +109,31 @@ def tile_trianglemultiplication_pa_kernel(tc, a_gated, b_gated, mask, norm_out_w
             )
             return raw
 
-        def regroup(dst, raw, on_vector):
+        def words_of_a(s1, raw, on_vector):
             if on_vector:
                 nc.vector.tensor_copy(
-                    out=dst.rearrange("p (c i) r (u e) -> p c (r u) i e", i=RUN_V, e=2),
-                    in_=raw[:].rearrange("p r (u e) (c i) -> p c (r u) i e", i=RUN_V, e=2),
+                    out=s1[:].rearrange("p r (c i) t -> p r c t i", i=RUN),
+                    in_=raw[:].rearrange("p r t (c i) -> p r c t i", i=RUN),
                 )
             else:
-                nc.scalar.copy(
-                    out=dst.rearrange("p (c i) r t -> p c (r t) i", i=RUN_S),
-                    in_=raw[:].rearrange("p r t (c i) -> p c (r t) i", i=RUN_S),
+                for r in range(CH):
+                    nc.scalar.copy(
+                        out=s1[:, r, :, :].rearrange("p (c i) t -> p c t i", i=RUN),
+                        in_=raw[:, r, :, :].rearrange("p t (c i) -> p c t i", i=RUN),
+                    )
+
+        def words_of_b(gb, j0, raw, on_vector):
+            if on_vector:
+                nc.vector.tensor_copy(
+                    out=gb[:, :, j0 : j0 + CH, :, :].rearrange("p g r q t -> p r g t q"),
+                    in_=raw[:].rearrange("p r t (g q) -> p r g t q", q=DBANK),
                 )
+            else:
+                for r in range(CH):
+                    nc.scalar.copy(
+                        out=gb[:, :, j0 + r, :, :].rearrange("p g q t -> p g t q"),
+                        in_=raw[:, r, :, :].rearrange("p t (g q) -> p g t q", q=DBANK),
+                    )
 
         for ih in range(NI // IH):
             ga = grp.tile([P, ND, IH, PACK], BF16, name="ga%d" % ih, offset=0, align_bytes=64)
@@ -116,27 +141,17 @@ def tile_trianglemultiplication_pa_kernel(tc, a_gated, b_gated, mask, norm_out_w
                 n = ih * (IH // CH) + c
                 i0 = n * CH
                 raw = load(a_gated, i0, ring, RAW_SLOTS_A[n % len(RAW_SLOTS_A)] * SLOT_BYTES, "raw_a%d" % n)
-                s1_shape = [P, ND, CH, PACK] if c in VECTOR_S1_A[ih] else [P, CH, ND, PACK]
                 s1 = ring.tile(
-                    s1_shape,
+                    [P, CH, ND, PACK],
                     BF16,
                     name="s1_%d" % n,
                     offset=S1_SLOTS_A[n % len(S1_SLOTS_A)] * SLOT_BYTES,
                     align_bytes=64,
                 )
-                if c in VECTOR_S1_A[ih]:
-                    regroup(s1[:], raw, True)
-                    in0 = s1[:]
-                else:
-                    for r in range(CH):
-                        nc.scalar.copy(
-                            out=s1[:, r, :, :].rearrange("p (c i) t -> p c t i", i=RUN_ROW),
-                            in_=raw[:, r, :, :].rearrange("p t (c i) -> p c t i", i=RUN_ROW),
-                        )
-                    in0 = s1[:].rearrange("p r d t -> p d r t")
+                words_of_a(s1, raw, c in VECTOR_S1_A[ih])
                 nc.vector.tensor_tensor(
                     out=ga[:, :, c * CH : (c + 1) * CH, :],
-                    in0=in0,
+                    in0=s1[:].rearrange("p r d t -> p d r t"),
                     in1=mask_pit[:, i0 : i0 + CH, :].unsqueeze(1).to_broadcast([P, ND, CH, PACK]),
                     op=ALU.mult,
                 )
@@ -149,9 +164,9 @@ def tile_trianglemultiplication_pa_kernel(tc, a_gated, b_gated, mask, norm_out_w
 
         for h in range(NJ // JH):
             if h == 0:
-                gb = ring.tile([P, ND, JH, PACK], BF16, name="gb0", offset=GB0_SLOT * SLOT_BYTES, align_bytes=64)
+                gb = ring.tile([P, NG, JH, DBANK, PACK], BF16, name="gb0", offset=GB0_SLOT * SLOT_BYTES, align_bytes=64)
             else:
-                gb = grp.tile([P, ND, JH, PACK], BF16, name="gb1", offset=0, align_bytes=64)
+                gb = grp.tile([P, NG, JH, DBANK, PACK], BF16, name="gb1", offset=0, align_bytes=64)
             for c in range(JH // CH):
                 if h == 0:
                     pool, offset = ring, RAW_SLOTS_B0[c] * SLOT_BYTES
@@ -160,13 +175,13 @@ def tile_trianglemultiplication_pa_kernel(tc, a_gated, b_gated, mask, norm_out_w
                 else:
                     pool, offset = grp, ND * JH * PACK * 2 + (c - len(RAW_SLOTS_B1)) * SLOT_BYTES
                 raw = load(b_gated, h * JH + c * CH, pool, offset, "raw_b%d_%d" % (h, c))
-                regroup(gb[:, :, c * CH : (c + 1) * CH, :], raw, c in VECTOR_S1_B[h])
-            dq = QW // (JH * PACK)
-            for d0 in range(0, ND, dq):
+                words_of_b(gb, c * CH, raw, c in VECTOR_S1_B[h])
+            gq = QW // (JH * DBANK * PACK)
+            for g0 in range(0, NG, gq):
                 nc.vector.quantize_mx(
-                    out=b_codes[h][:, d0 : d0 + dq, :].rearrange("p d j -> p (d j)").bitcast(FP8X4),
-                    scales=b_scales[h][:, d0 : d0 + dq, :].rearrange("p d j -> p (d j)"),
-                    in_=gb[:, d0 : d0 + dq, :, :].rearrange("p d r t -> p (d r t)"),
+                    out=b_codes[h][:, g0 : g0 + gq, :].rearrange("p g w -> p (g w)").bitcast(FP8X4),
+                    scales=b_scales[h][:, g0 : g0 + gq, :].rearrange("p g w -> p (g w)"),
+                    in_=gb[:, g0 : g0 + gq, :, :, :].rearrange("p g r q t -> p (g r q t)"),
                 )
 
         t_sb0 = grp.tile([P, JH, ND], F32, name="t_sb0", offset=12 * SLOT_BYTES, align_bytes=64)
@@ -175,23 +190,23 @@ def tile_trianglemultiplication_pa_kernel(tc, a_gated, b_gated, mask, norm_out_w
 
         def products(h, banks):
             for bank in banks:
-                d0 = bank * DBANK
-                acc = psum.tile([P, DBANK * DBANK * JH], F32, tag="bank")
+                g0 = bank // DBANK * DBANK
+                q = bank % DBANK
+                acc = psum.tile([P, DBANK, JH, DBANK], F32, tag="bank")
                 for s in range(DBANK):
+                    d = DBANK * (g0 + s) + q
                     nc.tensor.matmul_mx(
-                        out=acc[:, s * DBANK * JH : (s + 1) * DBANK * JH],
-                        lhsT=a_codes[:, d0 + s, :].bitcast(FP8X4),
-                        lhsT_scale=a_scales[:, d0 + s, :],
-                        rhs=b_codes[h][:, d0 : d0 + DBANK, :].rearrange("p d j -> p (d j)").bitcast(FP8X4),
-                        rhs_scale=b_scales[h][:, d0 : d0 + DBANK, :].rearrange("p d j -> p (d j)"),
+                        out=acc[:, s, :, :].rearrange("p j c -> p (j c)"),
+                        lhsT=a_codes[:, d, :].bitcast(FP8X4),
+                        lhsT_scale=a_scales[:, d, :],
+                        rhs=b_codes[h][:, g0 + s, :].bitcast(FP8X4),
+                        rhs_scale=b_scales[h][:, g0 + s, :],
                         start=True,
                         stop=True,
                     )
+                place = q * NG + g0
                 nc.scalar.copy(
-                    out=t_sb[h][:, :, d0 : d0 + DBANK],
-                    in_=acc[:]
-                    .rearrange("p (c j) -> p c j", j=JH)[:, 0 : DBANK * DBANK : DBANK + 1, :]
-                    .rearrange("p s j -> p j s"),
+                    out=t_sb[h][:, :, place : place + DBANK], in_=acc[:, :, :, q].rearrange("p s j -> p j s")
                 )
 
         late_offset = [(GB0_SLOT + 6) * SLOT_BYTES]
@@ -282,7 +297,7 @@ def tile_trianglemultiplication_pa_kernel(tc, a_gated, b_gated, mask, norm_out_w
         def turn_back(h, g):
             bank = psum.tile([P, JG, P], F32, tag="bank")
             for n in range(JG):
-                nc.tensor.transpose(bank[:, n, :], scaled[h, g][:, n, :], ident_f32[:])
+                nc.tensor.transpose(bank[:, n, :], scaled[h, g][:, n, :], unplace[:])
             back[h, g] = bank
 
         def out_of_psum_and_store(h, g):

@@ -32,12 +32,10 @@ GB0_SLOT = 0
 RAW_SLOTS_B0 = (8, 9, 18, 19, 20, 21, 10, 11)
 RAW_SLOTS_B1 = (8, 9, 10, 11)
 
-VECTOR_S1_A = ((0, 1, 3, 5, 9, 11), (10, 14))
-VECTOR_S1_B = ((6, 7), (1, 3, 5, 7))
+VECTOR_S1_A = ((1, 2, 4, 6, 9, 11), (10, 14))
+VECTOR_S1_B = ((0, 1), (1, 3, 4, 5, 7))
 JG = 4
 SCALED_BUFS = 4
-VECTOR_FROM_GROUP = 4
-ROOT0_AFTER_BANK = 25
 
 
 def tile_trianglemultiplication_pa_kernel(tc, a_gated, b_gated, mask, norm_out_w, norm_out_b, out):
@@ -68,7 +66,7 @@ def tile_trianglemultiplication_pa_kernel(tc, a_gated, b_gated, mask, norm_out_w
         eps_t = small.tile([P, 1], F32)
         nc.vector.memset(eps_t[:], EPS)
         warm = small.tile([P, 1], F32)
-        nc.scalar.activation(out=warm[:], in_=eps_t[:], func=ACT.Sqrt)
+        nc.scalar.activation(out=warm[:], in_=eps_t[:], func=ACT.Abs_reciprocal_sqrt)
 
         ident = small.tile([P, P], BF16)
         make_identity(nc, ident[:])
@@ -83,30 +81,15 @@ def tile_trianglemultiplication_pa_kernel(tc, a_gated, b_gated, mask, norm_out_w
         wb16 = small.tile([P, 2, ND], BF16)
         nc.scalar.dma_start(out=wb16[:, 0, :], in_=norm_out_w.partition_broadcast(P))
         nc.scalar.dma_start(out=wb16[:, 1, :], in_=norm_out_b.partition_broadcast(P))
-        wb16_placed = small.tile([P, 2, ND], BF16)
-        nc.vector.tensor_copy(
-            out=wb16_placed[:].rearrange("p n (q g) -> p n q g", q=DBANK),
-            in_=wb16[:].rearrange("p n (g q) -> p n q g", q=DBANK),
-        )
-        wb_ps = psum.tile([P, 2, P], BF16, tag="bank")
-        for n in range(2):
-            nc.tensor.transpose(wb_ps[:, n, :], wb16_placed[:, n, :], ident[:])
-        wb_col = small.tile([P, 2], F32)
-        nc.vector.tensor_copy(out=wb_col[:], in_=wb_ps[:, :, 0])
         ident_f32 = small.tile([P, P], F32)
         make_identity(nc, ident_f32[:])
-        unplace = small.tile([P, P], F32)
-        nc.vector.tensor_copy(
-            out=unplace[:].rearrange("p (g q) -> p q g", q=DBANK),
-            in_=ident_f32[:].rearrange("p (q g) -> p q g", q=DBANK),
-        )
-
-        def load(src, r0, pool, offset, name):
+        def load(src, r0, pool, offset, name, rows=CH):
             raw = pool.tile([P, CH, PACK, ND], BF16, name=name, offset=offset, align_bytes=64)
-            nc.sync.dma_start(
-                out=raw[:].rearrange("p r t d -> p r (t d)"),
-                in_=src[r0 : r0 + CH].rearrange("r (p t) d -> p r (t d)", t=PACK),
-            )
+            for r in range(0, CH, rows):
+                nc.sync.dma_start(
+                    out=raw[:, r : r + rows, :, :].rearrange("p r t d -> p r (t d)"),
+                    in_=src[r0 + r : r0 + r + rows].rearrange("r (p t) d -> p r (t d)", t=PACK),
+                )
             return raw
 
         def words_of_a(s1, raw, on_vector):
@@ -140,7 +123,7 @@ def tile_trianglemultiplication_pa_kernel(tc, a_gated, b_gated, mask, norm_out_w
             for c in range(IH // CH):
                 n = ih * (IH // CH) + c
                 i0 = n * CH
-                raw = load(a_gated, i0, ring, RAW_SLOTS_A[n % len(RAW_SLOTS_A)] * SLOT_BYTES, "raw_a%d" % n)
+                raw = load(a_gated, i0, ring, RAW_SLOTS_A[n % len(RAW_SLOTS_A)] * SLOT_BYTES, "raw_a%d" % n, 1 if n == 0 else CH)
                 s1 = ring.tile(
                     [P, CH, ND, PACK],
                     BF16,
@@ -155,6 +138,11 @@ def tile_trianglemultiplication_pa_kernel(tc, a_gated, b_gated, mask, norm_out_w
                     in1=mask_pit[:, i0 : i0 + CH, :].unsqueeze(1).to_broadcast([P, ND, CH, PACK]),
                     op=ALU.mult,
                 )
+            if ih == NI // IH - 1:
+                gb0 = ring.tile([P, NG, JH, DBANK, PACK], BF16, name="gb0", offset=GB0_SLOT * SLOT_BYTES, align_bytes=64)
+                for c in range(JH // CH):
+                    raw = load(b_gated, c * CH, ring, RAW_SLOTS_B0[c] * SLOT_BYTES, "raw_b0_%d" % c)
+                    words_of_b(gb0, c * CH, raw, c in VECTOR_S1_B[0])
             for d in range(ND):
                 nc.vector.quantize_mx(
                     out=a_codes[:, d, ih * IH : (ih + 1) * IH].bitcast(FP8X4),
@@ -162,31 +150,24 @@ def tile_trianglemultiplication_pa_kernel(tc, a_gated, b_gated, mask, norm_out_w
                     in_=ga[:, d, :, :].rearrange("p r t -> p (r t)"),
                 )
 
-        for h in range(NJ // JH):
-            if h == 0:
-                gb = ring.tile([P, NG, JH, DBANK, PACK], BF16, name="gb0", offset=GB0_SLOT * SLOT_BYTES, align_bytes=64)
-            else:
-                gb = grp.tile([P, NG, JH, DBANK, PACK], BF16, name="gb1", offset=0, align_bytes=64)
-            for c in range(JH // CH):
-                if h == 0:
-                    pool, offset = ring, RAW_SLOTS_B0[c] * SLOT_BYTES
-                elif c < len(RAW_SLOTS_B1):
-                    pool, offset = ring, RAW_SLOTS_B1[c] * SLOT_BYTES
-                else:
-                    pool, offset = grp, ND * JH * PACK * 2 + (c - len(RAW_SLOTS_B1)) * SLOT_BYTES
-                raw = load(b_gated, h * JH + c * CH, pool, offset, "raw_b%d_%d" % (h, c))
-                words_of_b(gb, c * CH, raw, c in VECTOR_S1_B[h])
-            gq = QW // (JH * DBANK * PACK)
-            for g0 in range(0, NG, gq):
-                nc.vector.quantize_mx(
-                    out=b_codes[h][:, g0 : g0 + gq, :].rearrange("p g w -> p (g w)").bitcast(FP8X4),
-                    scales=b_scales[h][:, g0 : g0 + gq, :].rearrange("p g w -> p (g w)"),
-                    in_=gb[:, g0 : g0 + gq, :, :, :].rearrange("p g r q t -> p (g r q t)"),
-                )
+        wb16_placed = small.tile([P, 2, ND], BF16)
+        nc.vector.tensor_copy(
+            out=wb16_placed[:].rearrange("p n (q g) -> p n q g", q=DBANK),
+            in_=wb16[:].rearrange("p n (g q) -> p n q g", q=DBANK),
+        )
+        wb_ps = psum.tile([P, 2, P], BF16, tag="bank")
+        for n in range(2):
+            nc.tensor.transpose(wb_ps[:, n, :], wb16_placed[:, n, :], ident[:])
+        wb_col = small.tile([P, 2], F32)
+        nc.vector.tensor_copy(out=wb_col[:], in_=wb_ps[:, :, 0])
+        unplace = small.tile([P, P], F32)
+        nc.vector.tensor_copy(
+            out=unplace[:].rearrange("p (g q) -> p q g", q=DBANK),
+            in_=ident_f32[:].rearrange("p (q g) -> p q g", q=DBANK),
+        )
 
         t_sb0 = grp.tile([P, JH, ND], F32, name="t_sb0", offset=12 * SLOT_BYTES, align_bytes=64)
-        t_sb1 = ring.tile([P, JH, ND], F32, name="t_sb1", offset=GB0_SLOT * SLOT_BYTES, align_bytes=64)
-        t_sb = [t_sb0, t_sb1]
+        t_sb = [t_sb0]
 
         def products(h, banks):
             for bank in banks:
@@ -209,6 +190,31 @@ def tile_trianglemultiplication_pa_kernel(tc, a_gated, b_gated, mask, norm_out_w
                     out=t_sb[h][:, :, place : place + DBANK], in_=acc[:, :, :, q].rearrange("p s j -> p j s")
                 )
 
+        for h in range(NJ // JH):
+            if h == 0:
+                gb = gb0
+            else:
+                gb = grp.tile([P, NG, JH, DBANK, PACK], BF16, name="gb1", offset=0, align_bytes=64)
+                for c in range(JH // CH):
+                    if c < len(RAW_SLOTS_B1):
+                        pool, offset = ring, RAW_SLOTS_B1[c] * SLOT_BYTES
+                    else:
+                        pool, offset = grp, ND * JH * PACK * 2 + (c - len(RAW_SLOTS_B1)) * SLOT_BYTES
+                    raw = load(b_gated, h * JH + c * CH, pool, offset, "raw_b%d_%d" % (h, c))
+                    words_of_b(gb, c * CH, raw, c in VECTOR_S1_B[h])
+            gq = QW // (JH * DBANK * PACK)
+            for g0 in range(0, NG, gq):
+                nc.vector.quantize_mx(
+                    out=b_codes[h][:, g0 : g0 + gq, :].rearrange("p g w -> p (g w)").bitcast(FP8X4),
+                    scales=b_scales[h][:, g0 : g0 + gq, :].rearrange("p g w -> p (g w)"),
+                    in_=gb[:, g0 : g0 + gq, :, :, :].rearrange("p g r q t -> p (g r q t)"),
+                )
+            if h == 0:
+                products(0, range(ND // DBANK))
+        t_sb1 = ring.tile([P, JH, ND], F32, name="t_sb1", offset=GB0_SLOT * SLOT_BYTES, align_bytes=64)
+        t_sb.append(t_sb1)
+
+
         late_offset = [(GB0_SLOT + 6) * SLOT_BYTES]
 
         def late_tile(shape, name):
@@ -220,58 +226,54 @@ def tile_trianglemultiplication_pa_kernel(tc, a_gated, b_gated, mask, norm_out_w
             return t
 
         stats = [late_tile([P, JH, 6], "stats%d" % h) for h in range(NJ // JH)]
-        mean2 = [late_tile([P, JH], "mean2_%d" % h) for h in range(NJ // JH)]
+        mean = [late_tile([P, JH], "mean%d" % h) for h in range(NJ // JH)]
         diff = [late_tile([P, JH], "diff%d" % h) for h in range(NJ // JH)]
+        diff2 = [late_tile([P, JH], "diff2_%d" % h) for h in range(NJ // JH)]
         m2 = [late_tile([P, JH], "m2_%d" % h) for h in range(NJ // JH)]
         var4 = [late_tile([P, JH], "var4_%d" % h) for h in range(NJ // JH)]
-        std = [late_tile([P, JH], "std%d" % h) for h in range(NJ // JH)]
         rstd = [late_tile([P, JH], "rstd%d" % h) for h in range(NJ // JH)]
-        shift = [late_tile([P, JH], "shift%d" % h) for h in range(NJ // JH)]
 
-        def moments(h, j0=0, j1=JH):
+        def row_stats(h, j0, j1):
             for j in range(j0, j1):
                 nc.vector.bn_stats(out=stats[h][:, j, :], in_=t_sb[h][:, j, :])
+
+        def variance_steps(h, j0, j1):
             st = stats[h][:, j0:j1, :]
             js = slice(j0, j1)
-            nc.vector.tensor_tensor(out=mean2[h][:, js], in0=st[:, :, 1], in1=st[:, :, 4], op=ALU.add)
-            nc.vector.tensor_tensor(out=diff[h][:, js], in0=st[:, :, 1], in1=st[:, :, 4], op=ALU.subtract)
-            nc.vector.tensor_tensor(out=m2[h][:, js], in0=st[:, :, 2], in1=st[:, :, 5], op=ALU.add)
-            nc.vector.tensor_tensor(out=diff[h][:, js], in0=diff[h][:, js], in1=diff[h][:, js], op=ALU.mult)
-            nc.vector.scalar_tensor_tensor(
-                out=var4[h][:, js], in0=m2[h][:, js], scalar=1.0 / 32.0, in1=diff[h][:, js], op0=ALU.mult, op1=ALU.add
+            return (
+                lambda: nc.vector.tensor_tensor(out=diff[h][:, js], in0=st[:, :, 1], in1=st[:, :, 4], op=ALU.subtract),
+                lambda: nc.vector.scalar_tensor_tensor(
+                    out=mean[h][:, js], in0=diff[h][:, js], scalar=0.5, in1=st[:, :, 4], op0=ALU.mult, op1=ALU.add
+                ),
+                lambda: nc.vector.tensor_tensor(out=m2[h][:, js], in0=st[:, :, 2], in1=st[:, :, 5], op=ALU.add),
+                lambda: nc.vector.tensor_tensor(
+                    out=diff2[h][:, js], in0=diff[h][:, js], in1=diff[h][:, js], op=ALU.mult
+                ),
+                lambda: nc.vector.scalar_tensor_tensor(
+                    out=var4[h][:, js],
+                    in0=m2[h][:, js],
+                    scalar=1.0 / 32.0,
+                    in1=diff2[h][:, js],
+                    op0=ALU.mult,
+                    op1=ALU.add,
+                ),
             )
 
-        def root(h, j0=0, j1=JH):
-            nc.scalar.activation(
-                out=std[h][:, j0:j1], in_=var4[h][:, j0:j1], func=ACT.Sqrt, scale=0.25, bias=eps_t[:, 0:1]
-            )
-
-        def scale_and_shift(h, j0=0, j1=JH):
+        def root(h, j0, j1):
             js = slice(j0, j1)
-            nc.vector.reciprocal(out=rstd[h][:, js], in_=std[h][:, js])
-            nc.vector.scalar_tensor_tensor(
-                out=shift[h][:, js], in0=mean2[h][:, js], scalar=-0.5, in1=rstd[h][:, js], op0=ALU.mult, op1=ALU.mult
+            nc.scalar.activation(
+                out=rstd[h][:, js], in_=var4[h][:, js], func=ACT.Abs_reciprocal_sqrt, scale=0.25, bias=eps_t[:, 0:1]
             )
 
-        def normalise(h, js):
-            for j in js:
-                nc.scalar.activation(
-                    out=t_sb[h][:, j, :],
-                    in_=t_sb[h][:, j, :],
-                    func=ACT.Identity,
-                    scale=rstd[h][:, j : j + 1],
-                    bias=shift[h][:, j : j + 1],
-                )
-
-        def normalise_on_vector(h, js):
-            for j in js:
+        def normalise(h, j0, j1):
+            for j in range(j0, j1):
                 nc.vector.tensor_scalar(
                     out=t_sb[h][:, j, :],
                     in0=t_sb[h][:, j, :],
-                    scalar1=rstd[h][:, j : j + 1],
-                    scalar2=shift[h][:, j : j + 1],
-                    op0=ALU.mult,
-                    op1=ALU.add,
+                    scalar1=mean[h][:, j : j + 1],
+                    scalar2=rstd[h][:, j : j + 1],
+                    op0=ALU.subtract,
+                    op1=ALU.mult,
                 )
 
         turned = {}
@@ -300,49 +302,102 @@ def tile_trianglemultiplication_pa_kernel(tc, a_gated, b_gated, mask, norm_out_w
                 nc.tensor.transpose(bank[:, n, :], scaled[h, g][:, n, :], unplace[:])
             back[h, g] = bank
 
-        def out_of_psum_and_store(h, g):
-            nc.vector.tensor_copy(out=t_sb[h][:, g * JG : (g + 1) * JG, :], in_=back[h, g][:])
-            if g % 2 == 1:
-                j0 = (g - 1) * JG
-                nc.sync.dma_start(out=out[:, h * JH + j0 : h * JH + j0 + 2 * JG, :], in_=t_sb[h][:, j0 : j0 + 2 * JG, :])
+        def out_of_psum(copy, h, g):
+            copy(out=t_sb[h][:, g * JG : (g + 1) * JG, :], in_=back[h, g][:])
+
+        def store(h, g0, g1):
+            js = slice(g0 * JG, g1 * JG)
+            nc.sync.dma_start(out=out[:, h * JH + js.start : h * JH + js.stop, :], in_=t_sb[h][:, js, :])
 
         n_banks = ND // DBANK
-        n_groups = JH // JG
-        products(0, range(n_banks))
-        moments(0)
-        products(1, range(ROOT0_AFTER_BANK))
-        root(0)
-        products(1, range(ROOT0_AFTER_BANK, n_banks))
-        scale_and_shift(0)
-        normalise_on_vector(0, range(JH))
-        for g in range(n_groups):
-            turn(0, g)
+        on_vector = nc.vector.tensor_copy
+        on_scalar = nc.scalar.copy
         half = JH // 2
-        moments(1, 0, half)
-        for g in range(n_groups // 2):
-            gain_bias(0, g)
-            turn_back(0, g)
-        root(1, 0, half)
-        moments(1, half, JH)
-        scale_and_shift(1, 0, half)
-        for g in range(n_groups // 2, n_groups):
-            gain_bias(0, g)
-            turn_back(0, g)
-        root(1, half, JH)
-        out_of_psum_and_store(0, 0)
-        out_of_psum_and_store(0, 1)
-        scale_and_shift(1, half, JH)
-        for g in range(2, n_groups):
-            out_of_psum_and_store(0, g)
-        normalise_on_vector(1, range(VECTOR_FROM_GROUP * JG, JH))
-        for s in range(n_groups + 4):
-            if s < VECTOR_FROM_GROUP:
-                normalise(1, range(s * JG, (s + 1) * JG))
-            if 0 <= s - 1 < n_groups:
-                turn(1, s - 1)
-            if 0 <= s - 2 < n_groups:
-                gain_bias(1, s - 2)
-            if 0 <= s - 3 < n_groups:
-                turn_back(1, s - 3)
-            if 0 <= s - 4 < n_groups:
-                out_of_psum_and_store(1, s - 4)
+
+        def woven(steps, h, j):
+            steps[0]()
+            row_stats(h, j, j + 1)
+            steps[1]()
+            steps[2]()
+            row_stats(h, j + 1, j + 2)
+            steps[3]()
+            row_stats(h, j + 2, j + 3)
+            steps[4]()
+            row_stats(h, j + 3, j + 4)
+
+        def gains(h, g0, g1):
+            for g in range(g0, g1):
+                gain_bias(h, g)
+
+        with tc.manual_schedule(
+            engines={mybir.EngineType.PE, mybir.EngineType.Activation, mybir.EngineType.DVE}
+        ):
+            products(1, range(0, 20))
+            row_stats(0, 0, half)
+            woven(variance_steps(0, 0, half), 0, half)
+            root(0, 0, half)
+            row_stats(0, half + 4, half + 7)
+            normalise(0, 0, half)
+            row_stats(0, half + 7, JH)
+            products(1, range(20, n_banks))
+            for g in range(4):
+                turn(0, g)
+            gains(0, 0, 2)
+            woven(variance_steps(0, half, JH), 1, 0)
+            root(0, half, JH)
+            row_stats(1, 4, 7)
+            normalise(0, half, JH)
+            row_stats(1, 7, half)
+            gains(0, 2, 4)
+            for g in range(4):
+                turn_back(0, g)
+            for g in range(4, 8):
+                turn(0, g)
+            out_of_psum(on_scalar, 0, 0)
+            gains(0, 4, 6)
+            woven(variance_steps(1, 0, half), 1, half)
+            root(1, 0, half)
+            gains(0, 6, 8)
+            for g in range(4, 8):
+                turn_back(0, g)
+            row_stats(1, half + 4, half + 7)
+            normalise(1, 0, half)
+            row_stats(1, half + 7, JH)
+            out_of_psum(on_scalar, 0, 1)
+            store(0, 0, 2)
+            out_of_psum(on_scalar, 0, 2)
+            for g in range(4):
+                turn(1, g)
+            out_of_psum(on_scalar, 0, 3)
+            store(0, 2, 4)
+            steps = variance_steps(1, half, JH)
+            for step in steps[:4]:
+                step()
+            out_of_psum(on_vector, 0, 4)
+            steps[4]()
+            out_of_psum(on_vector, 0, 5)
+            store(0, 4, 6)
+            gains(1, 0, 2)
+            root(1, half, JH)
+            normalise(1, half, JH)
+            gains(1, 2, 4)
+            for g in range(4):
+                turn_back(1, g)
+            out_of_psum(on_scalar, 0, 6)
+            out_of_psum(on_scalar, 0, 7)
+            store(0, 6, 8)
+            for g in range(4, 8):
+                turn(1, g)
+            for g in range(4):
+                out_of_psum(on_vector, 1, g)
+            store(1, 0, 2)
+            store(1, 2, 4)
+            for g in range(4, 8):
+                gain_bias(1, g)
+                turn_back(1, g)
+            out_of_psum(on_vector, 1, 4)
+            out_of_psum(on_vector, 1, 5)
+            store(1, 4, 6)
+            out_of_psum(on_scalar, 1, 6)
+            out_of_psum(on_vector, 1, 7)
+            store(1, 6, 8)

@@ -35,6 +35,7 @@ RAW_SLOTS_B1 = (8, 9, 10, 11)
 VECTOR_S1_A = ((1, 2, 4, 6, 9, 11), (10, 14))
 VECTOR_S1_B = ((0, 1), (1, 3, 4, 5, 7))
 JG = 4
+BATCH = 8
 SCALED_BUFS = 4
 
 
@@ -225,60 +226,40 @@ def tile_trianglemultiplication_pa_kernel(tc, a_gated, b_gated, mask, norm_out_w
             late_offset[0] += (size + 63) // 64 * 64
             return t
 
-        stats = [late_tile([P, JH, 6], "stats%d" % h) for h in range(NJ // JH)]
-        mean = [late_tile([P, JH], "mean%d" % h) for h in range(NJ // JH)]
-        diff = [late_tile([P, JH], "diff%d" % h) for h in range(NJ // JH)]
-        diff2 = [late_tile([P, JH], "diff2_%d" % h) for h in range(NJ // JH)]
-        m2 = [late_tile([P, JH], "m2_%d" % h) for h in range(NJ // JH)]
-        var4 = [late_tile([P, JH], "var4_%d" % h) for h in range(NJ // JH)]
-        rstd = [late_tile([P, JH], "rstd%d" % h) for h in range(NJ // JH)]
+        stats = [late_tile([P, JH // 2, 2, 3], "stats%d" % h) for h in range(NJ // JH)]
+        rstd = [late_tile([P, JH // 2, 2], "rstd%d" % h) for h in range(NJ // JH)]
 
-        def row_stats(h, j0, j1):
-            for j in range(j0, j1):
-                nc.vector.bn_stats(out=stats[h][:, j, :], in_=t_sb[h][:, j, :])
+        def moments(h, k):
+            for n in range(k * BATCH // 2, (k + 1) * BATCH // 2):
+                nc.vector.bn_stats(
+                    out=stats[h][:, n, :, :].rearrange("p e s -> p (e s)"),
+                    in_=t_sb[h][:, 2 * n : 2 * n + 2, :].rearrange("p e d -> p d e"),
+                )
 
-        def variance_steps(h, j0, j1):
-            st = stats[h][:, j0:j1, :]
-            js = slice(j0, j1)
-            return (
-                lambda: nc.vector.tensor_tensor(out=diff[h][:, js], in0=st[:, :, 1], in1=st[:, :, 4], op=ALU.subtract),
-                lambda: nc.vector.scalar_tensor_tensor(
-                    out=mean[h][:, js], in0=diff[h][:, js], scalar=0.5, in1=st[:, :, 4], op0=ALU.mult, op1=ALU.add
-                ),
-                lambda: nc.vector.tensor_tensor(out=m2[h][:, js], in0=st[:, :, 2], in1=st[:, :, 5], op=ALU.add),
-                lambda: nc.vector.tensor_tensor(
-                    out=diff2[h][:, js], in0=diff[h][:, js], in1=diff[h][:, js], op=ALU.mult
-                ),
-                lambda: nc.vector.scalar_tensor_tensor(
-                    out=var4[h][:, js],
-                    in0=m2[h][:, js],
-                    scalar=1.0 / 32.0,
-                    in1=diff2[h][:, js],
-                    op0=ALU.mult,
-                    op1=ALU.add,
-                ),
-            )
-
-        def root(h, j0, j1):
-            js = slice(j0, j1)
+        def root(h, k):
+            ns = slice(k * BATCH // 2, (k + 1) * BATCH // 2)
             nc.scalar.activation(
-                out=rstd[h][:, js], in_=var4[h][:, js], func=ACT.Abs_reciprocal_sqrt, scale=0.25, bias=eps_t[:, 0:1]
+                out=rstd[h][:, ns, :],
+                in_=stats[h][:, ns, :, 2],
+                func=ACT.Abs_reciprocal_sqrt,
+                scale=1.0 / ND,
+                bias=eps_t[:, 0:1],
             )
 
-        def normalise(h, j0, j1):
-            for j in range(j0, j1):
+        def normalise(h, k):
+            for j in range(k * BATCH, (k + 1) * BATCH):
+                n, e = j // 2, j % 2
                 nc.vector.tensor_scalar(
                     out=t_sb[h][:, j, :],
                     in0=t_sb[h][:, j, :],
-                    scalar1=mean[h][:, j : j + 1],
-                    scalar2=rstd[h][:, j : j + 1],
+                    scalar1=stats[h][:, n, e, 1:2],
+                    scalar2=rstd[h][:, n, e : e + 1],
                     op0=ALU.subtract,
                     op1=ALU.mult,
                 )
 
         turned = {}
         scaled = {}
-        back = {}
         n_scaled = [0]
 
         def turn(h, g):
@@ -297,13 +278,11 @@ def tile_trianglemultiplication_pa_kernel(tc, a_gated, b_gated, mask, norm_out_w
             scaled[h, g] = tile
 
         def turn_back(h, g):
-            bank = psum.tile([P, JG, P], F32, tag="bank")
             for n in range(JG):
-                nc.tensor.transpose(bank[:, n, :], scaled[h, g][:, n, :], unplace[:])
-            back[h, g] = bank
+                nc.tensor.transpose(turned[h, g][:, n, :], scaled[h, g][:, n, :], unplace[:])
 
         def out_of_psum(copy, h, g):
-            copy(out=t_sb[h][:, g * JG : (g + 1) * JG, :], in_=back[h, g][:])
+            copy(out=t_sb[h][:, g * JG : (g + 1) * JG, :], in_=turned[h, g][:])
 
         def store(h, g0, g1):
             js = slice(g0 * JG, g1 * JG)
@@ -312,92 +291,107 @@ def tile_trianglemultiplication_pa_kernel(tc, a_gated, b_gated, mask, norm_out_w
         n_banks = ND // DBANK
         on_vector = nc.vector.tensor_copy
         on_scalar = nc.scalar.copy
-        half = JH // 2
-
-        def woven(steps, h, j):
-            steps[0]()
-            row_stats(h, j, j + 1)
-            steps[1]()
-            steps[2]()
-            row_stats(h, j + 1, j + 2)
-            steps[3]()
-            row_stats(h, j + 2, j + 3)
-            steps[4]()
-            row_stats(h, j + 3, j + 4)
-
-        def gains(h, g0, g1):
-            for g in range(g0, g1):
-                gain_bias(h, g)
 
         with tc.manual_schedule(
             engines={mybir.EngineType.PE, mybir.EngineType.Activation, mybir.EngineType.DVE}
         ):
-            products(1, range(0, 20))
-            row_stats(0, 0, half)
-            woven(variance_steps(0, 0, half), 0, half)
-            root(0, 0, half)
-            row_stats(0, half + 4, half + 7)
-            normalise(0, 0, half)
-            row_stats(0, half + 7, JH)
-            products(1, range(20, n_banks))
-            for g in range(4):
-                turn(0, g)
-            gains(0, 0, 2)
-            woven(variance_steps(0, half, JH), 1, 0)
-            root(0, half, JH)
-            row_stats(1, 4, 7)
-            normalise(0, half, JH)
-            row_stats(1, 7, half)
-            gains(0, 2, 4)
-            for g in range(4):
-                turn_back(0, g)
-            for g in range(4, 8):
-                turn(0, g)
+            products(1, range(0, 18))
+            moments(0, 0)
+            root(0, 0)
+            products(1, range(18, 22))
+            moments(0, 1)
+            root(0, 1)
+            normalise(0, 0)
+            products(1, range(22, 27))
+            moments(0, 2)
+            root(0, 2)
+            normalise(0, 1)
+            products(1, range(27, n_banks))
+            moments(0, 3)
+            root(0, 3)
+            normalise(0, 2)
+            turn(0, 0)
+            turn(0, 1)
+            turn(0, 2)
+            turn(0, 3)
+            gain_bias(0, 0)
+            turn_back(0, 0)
+            gain_bias(0, 1)
+            turn_back(0, 1)
+            moments(1, 0)
+            root(1, 0)
+            normalise(0, 3)
+            moments(1, 1)
+            turn(0, 4)
+            turn(0, 5)
+            gain_bias(0, 2)
+            turn_back(0, 2)
+            gain_bias(0, 3)
+            turn_back(0, 3)
+            root(1, 1)
+            normalise(1, 0)
+            turn(0, 6)
+            turn(0, 7)
+            gain_bias(0, 4)
+            turn_back(0, 4)
             out_of_psum(on_scalar, 0, 0)
-            gains(0, 4, 6)
-            woven(variance_steps(1, 0, half), 1, half)
-            root(1, 0, half)
-            gains(0, 6, 8)
-            for g in range(4, 8):
-                turn_back(0, g)
-            row_stats(1, half + 4, half + 7)
-            normalise(1, 0, half)
-            row_stats(1, half + 7, JH)
+            turn(1, 0)
+            gain_bias(0, 5)
+            turn_back(0, 5)
             out_of_psum(on_scalar, 0, 1)
             store(0, 0, 2)
+            turn(1, 1)
+            moments(1, 2)
+            normalise(1, 1)
+            root(1, 2)
+            gain_bias(0, 6)
+            turn_back(0, 6)
+            gain_bias(0, 7)
+            turn_back(0, 7)
+            moments(1, 3)
             out_of_psum(on_scalar, 0, 2)
-            for g in range(4):
-                turn(1, g)
-            out_of_psum(on_scalar, 0, 3)
+            turn(1, 2)
+            root(1, 3)
+            normalise(1, 2)
+            gain_bias(1, 0)
+            turn_back(1, 0)
+            gain_bias(1, 1)
+            turn_back(1, 1)
+            normalise(1, 3)
+            out_of_psum(on_vector, 0, 3)
             store(0, 2, 4)
-            steps = variance_steps(1, half, JH)
-            for step in steps[:4]:
-                step()
+            turn(1, 3)
             out_of_psum(on_vector, 0, 4)
-            steps[4]()
+            turn(1, 4)
+            gain_bias(1, 2)
+            turn_back(1, 2)
+            gain_bias(1, 3)
+            turn_back(1, 3)
             out_of_psum(on_vector, 0, 5)
             store(0, 4, 6)
-            gains(1, 0, 2)
-            root(1, half, JH)
-            normalise(1, half, JH)
-            gains(1, 2, 4)
-            for g in range(4):
-                turn_back(1, g)
-            out_of_psum(on_scalar, 0, 6)
-            out_of_psum(on_scalar, 0, 7)
+            turn(1, 5)
+            out_of_psum(on_vector, 0, 6)
+            turn(1, 6)
+            out_of_psum(on_vector, 0, 7)
             store(0, 6, 8)
-            for g in range(4, 8):
-                turn(1, g)
-            for g in range(4):
-                out_of_psum(on_vector, 1, g)
+            turn(1, 7)
+            gain_bias(1, 4)
+            turn_back(1, 4)
+            gain_bias(1, 5)
+            turn_back(1, 5)
+            out_of_psum(on_vector, 1, 0)
+            gain_bias(1, 6)
+            turn_back(1, 6)
+            gain_bias(1, 7)
+            turn_back(1, 7)
+            out_of_psum(on_vector, 1, 1)
             store(1, 0, 2)
+            out_of_psum(on_vector, 1, 2)
+            out_of_psum(on_scalar, 1, 3)
             store(1, 2, 4)
-            for g in range(4, 8):
-                gain_bias(1, g)
-                turn_back(1, g)
             out_of_psum(on_vector, 1, 4)
-            out_of_psum(on_vector, 1, 5)
+            out_of_psum(on_scalar, 1, 5)
             store(1, 4, 6)
-            out_of_psum(on_scalar, 1, 6)
-            out_of_psum(on_vector, 1, 7)
+            out_of_psum(on_vector, 1, 6)
+            out_of_psum(on_scalar, 1, 7)
             store(1, 6, 8)

@@ -25,15 +25,15 @@ QW = 4096
 RUN = 8
 NG = ND // 4
 SLOT_BYTES = CH * PACK * ND * 2
-CODE_SLOT = 12
 RAW_SLOTS_A = tuple(range(0, 10))
 S1_SLOTS_A = tuple(range(10, 22))
 GB0_SLOT = 0
-RAW_SLOTS_B0 = (8, 9, 18, 19, 20, 21, 10, 11)
-RAW_SLOTS_B1 = (8, 9, 10, 11)
+GB1_SLOT = 8
+RAW_SLOTS_B0 = (8, 9, 18, 19, 20, 21, 16, 17)
+RAW_SLOTS_B1 = (18, 19, 20, None, None, 21, 16, 17)
 
-VECTOR_S1_A = ((1, 2, 4, 6, 9, 11), (10, 14))
-VECTOR_S1_B = ((0, 1), (1, 3, 4, 5, 7))
+VECTOR_S1_A = ((1, 4, 7, 9, 12, 14), (5, 9))
+VECTOR_S1_B = ((0,), (3, 4, 5, 6, 7))
 JG = 4
 BATCH = 8
 SCALED_BUFS = 4
@@ -50,17 +50,6 @@ def tile_trianglemultiplication_pa_kernel(tc, a_gated, b_gated, mask, norm_out_w
 
         a_codes = keep.tile([P, ND, NI], U32, align_bytes=64)
         a_scales = keep.tile([P, ND, NI], U8, align_bytes=64)
-        b_base = CODE_SLOT * SLOT_BYTES
-        b_codes = [
-            ring.tile([P, NG, JH * DBANK], U32, name="b_codes%d" % h, offset=b_base + h * ND * JH * 4, align_bytes=64)
-            for h in range(NJ // JH)
-        ]
-        b_scales = [
-            ring.tile(
-                [P, NG, JH * DBANK], U8, name="b_scales%d" % h, offset=b_base + NJ * ND * 4 + h * ND * JH, align_bytes=64
-            )
-            for h in range(NJ // JH)
-        ]
         mask_ik = grp.tile([P, NK], BF16, offset=0, align_bytes=64)
         nc.scalar.dma_start(out=mask_ik[:], in_=mask)
 
@@ -79,9 +68,10 @@ def tile_trianglemultiplication_pa_kernel(tc, a_gated, b_gated, mask, norm_out_w
         mask_pit = small.tile([P, NI, PACK], BF16)
         nc.vector.tensor_copy(out=mask_pit[:], in_=mask_ps[:].rearrange("p t i -> p i t"))
 
-        wb16 = small.tile([P, 2, ND], BF16)
-        nc.scalar.dma_start(out=wb16[:, 0, :], in_=norm_out_w.partition_broadcast(P))
-        nc.scalar.dma_start(out=wb16[:, 1, :], in_=norm_out_b.partition_broadcast(P))
+        wb16 = small.tile([P, ND], BF16)
+        nc.vector.memset(wb16[:], 0.0)
+        nc.scalar.dma_start(out=wb16[0:1, :], in_=norm_out_w.unsqueeze(0))
+        nc.scalar.dma_start(out=wb16[1:2, :], in_=norm_out_b.unsqueeze(0))
         ident_f32 = small.tile([P, P], F32)
         make_identity(nc, ident_f32[:])
         def load(src, r0, pool, offset, name, rows=CH):
@@ -151,16 +141,15 @@ def tile_trianglemultiplication_pa_kernel(tc, a_gated, b_gated, mask, norm_out_w
                     in_=ga[:, d, :, :].rearrange("p r t -> p (r t)"),
                 )
 
-        wb16_placed = small.tile([P, 2, ND], BF16)
+        wb16_placed = small.tile([P, ND], BF16)
         nc.vector.tensor_copy(
-            out=wb16_placed[:].rearrange("p n (q g) -> p n q g", q=DBANK),
-            in_=wb16[:].rearrange("p n (g q) -> p n q g", q=DBANK),
+            out=wb16_placed[:].rearrange("p (q g) -> p q g", q=DBANK),
+            in_=wb16[:].rearrange("p (g q) -> p q g", q=DBANK),
         )
-        wb_ps = psum.tile([P, 2, P], BF16, tag="bank")
-        for n in range(2):
-            nc.tensor.transpose(wb_ps[:, n, :], wb16_placed[:, n, :], ident[:])
+        wb_ps = psum.tile([P, P], BF16, tag="bank")
+        nc.tensor.transpose(wb_ps[:], wb16_placed[:], ident[:])
         wb_col = small.tile([P, 2], F32)
-        nc.vector.tensor_copy(out=wb_col[:], in_=wb_ps[:, :, 0])
+        nc.vector.tensor_copy(out=wb_col[:], in_=wb_ps[:, 0:2])
         unplace = small.tile([P, P], F32)
         nc.vector.tensor_copy(
             out=unplace[:].rearrange("p (g q) -> p q g", q=DBANK),
@@ -191,16 +180,24 @@ def tile_trianglemultiplication_pa_kernel(tc, a_gated, b_gated, mask, norm_out_w
                     out=t_sb[h][:, :, place : place + DBANK], in_=acc[:, :, :, q].rearrange("p s j -> p j s")
                 )
 
+        b_codes = [
+            grp.tile([P, NG, JH * DBANK], U32, name="b_codes%d" % h, offset=h * ND * JH * 5, align_bytes=64)
+            for h in range(NJ // JH)
+        ]
+        b_scales = [
+            grp.tile([P, NG, JH * DBANK], U8, name="b_scales%d" % h, offset=h * ND * JH * 5 + ND * JH * 4, align_bytes=64)
+            for h in range(NJ // JH)
+        ]
         for h in range(NJ // JH):
             if h == 0:
                 gb = gb0
             else:
-                gb = grp.tile([P, NG, JH, DBANK, PACK], BF16, name="gb1", offset=0, align_bytes=64)
+                gb = ring.tile([P, NG, JH, DBANK, PACK], BF16, name="gb1", offset=GB1_SLOT * SLOT_BYTES, align_bytes=64)
                 for c in range(JH // CH):
-                    if c < len(RAW_SLOTS_B1):
+                    if RAW_SLOTS_B1[c] is not None:
                         pool, offset = ring, RAW_SLOTS_B1[c] * SLOT_BYTES
                     else:
-                        pool, offset = grp, ND * JH * PACK * 2 + (c - len(RAW_SLOTS_B1)) * SLOT_BYTES
+                        pool, offset = grp, ND * JH * 10 + c % 2 * SLOT_BYTES
                     raw = load(b_gated, h * JH + c * CH, pool, offset, "raw_b%d_%d" % (h, c))
                     words_of_b(gb, c * CH, raw, c in VECTOR_S1_B[h])
             gq = QW // (JH * DBANK * PACK)

from contextlib import ExitStack

import concourse.mybir as mybir
from concourse.masks import make_identity

FP8X4 = mybir.dt.float8_e4m3fn_x4
BF16 = mybir.dt.bfloat16
F32 = mybir.dt.float32
U32 = mybir.dt.uint32
U8 = mybir.dt.uint8
ALU = mybir.AluOpType
ACT = mybir.ActivationFunctionType

P = 128
PACK = 4
NI, NJ, NK, ND = 128, 64, 512, 128
EPS = 1e-5
FLOPS = 2 * NI * NJ * NK * ND

CH = 4
IH = 64
JH = 32
DBANK = 4
QW = 4096
RUN = 8
NG = ND // 4
SLOT_BYTES = CH * PACK * ND * 2
RAW_SLOTS_A = tuple(range(0, 10))
S1_SLOTS_A = tuple(range(10, 22))
GB0_SLOT = 0
GB1_SLOT = 8
RAW_SLOTS_B0 = (8, 9, 18, 19, 20, 21, 16, 17)
RAW_SLOTS_B1 = (18, 19, 20, None, None, 21, 16, 17)

VECTOR_S1_A = ((1, 4, 7, 9, 12, 14), (5, 9))
VECTOR_S1_B = ((0,), (3, 4, 5, 6, 7))
JG = 4
BATCH = 8
SCALED_BUFS = 4


def tile_trianglemultiplication_pa_kernel(tc, a_gated, b_gated, mask, norm_out_w, norm_out_b, out):
    nc = tc.nc
    with ExitStack() as ctx:
        keep = ctx.enter_context(tc.tile_pool(name="keep", bufs=1))
        small = ctx.enter_context(tc.tile_pool(name="small", bufs=1))
        ring = ctx.enter_context(tc.tile_pool(name="ring", bufs=1))
        grp = ctx.enter_context(tc.tile_pool(name="grp", bufs=1))
        psum = ctx.enter_context(tc.psum_pool(name="psum", bufs=8))

        a_codes = keep.tile([P, ND, NI], U32, align_bytes=64)
        a_scales = keep.tile([P, ND, NI], U8, align_bytes=64)
        mask_ik = grp.tile([P, NK], BF16, offset=0, align_bytes=64)
        nc.scalar.dma_start(out=mask_ik[:], in_=mask)

        eps_t = small.tile([P, 1], F32)
        nc.vector.memset(eps_t[:], EPS)
        warm = small.tile([P, 1], F32)
        nc.scalar.activation(out=warm[:], in_=eps_t[:], func=ACT.Abs_reciprocal_sqrt)

        ident = small.tile([P, P], BF16)
        make_identity(nc, ident[:])
        mask_itp = grp.tile([P, PACK, P], BF16, offset=NK * 2, align_bytes=64)
        nc.vector.tensor_copy(out=mask_itp[:], in_=mask_ik[:].rearrange("i (p t) -> i t p", t=PACK))
        mask_ps = psum.tile([P, PACK, P], BF16, tag="bank")
        for t in range(PACK):
            nc.tensor.transpose(mask_ps[:, t, :], mask_itp[:, t, :], ident[:])
        mask_pit = small.tile([P, NI, PACK], BF16)
        nc.vector.tensor_copy(out=mask_pit[:], in_=mask_ps[:].rearrange("p t i -> p i t"))

        wb16 = small.tile([P, ND], BF16)
        nc.vector.memset(wb16[:], 0.0)
        nc.scalar.dma_start(out=wb16[0:1, :], in_=norm_out_w.unsqueeze(0))
        nc.scalar.dma_start(out=wb16[1:2, :], in_=norm_out_b.unsqueeze(0))
        ident_f32 = small.tile([P, P], F32)
        make_identity(nc, ident_f32[:])
        def load(src, r0, pool, offset, name, rows=CH):
            raw = pool.tile([P, CH, PACK, ND], BF16, name=name, offset=offset, align_bytes=64)
            for r in range(0, CH, rows):
                nc.sync.dma_start(
                    out=raw[:, r : r + rows, :, :].rearrange("p r t d -> p r (t d)"),
                    in_=src[r0 + r : r0 + r + rows].rearrange("r (p t) d -> p r (t d)", t=PACK),
                )
            return raw

        def words_of_a(s1, raw, on_vector):
            if on_vector:
                nc.vector.tensor_copy(
                    out=s1[:].rearrange("p r (c i) t -> p r c t i", i=RUN),
                    in_=raw[:].rearrange("p r t (c i) -> p r c t i", i=RUN),
                )
            else:
                for r in range(CH):
                    nc.scalar.copy(
                        out=s1[:, r, :, :].rearrange("p (c i) t -> p c t i", i=RUN),
                        in_=raw[:, r, :, :].rearrange("p t (c i) -> p c t i", i=RUN),
                    )

        def words_of_b(gb, j0, raw, on_vector):
            if on_vector:
                nc.vector.tensor_copy(
                    out=gb[:, :, j0 : j0 + CH, :, :].rearrange("p g r q t -> p r g t q"),
                    in_=raw[:].rearrange("p r t (g q) -> p r g t q", q=DBANK),
                )
            else:
                for r in range(CH):
                    nc.scalar.copy(
                        out=gb[:, :, j0 + r, :, :].rearrange("p g q t -> p g t q"),
                        in_=raw[:, r, :, :].rearrange("p t (g q) -> p g t q", q=DBANK),
                    )

        for ih in range(NI // IH):
            ga = grp.tile([P, ND, IH, PACK], BF16, name="ga%d" % ih, offset=0, align_bytes=64)
            for c in range(IH // CH):
                n = ih * (IH // CH) + c
                i0 = n * CH
                raw = load(a_gated, i0, ring, RAW_SLOTS_A[n % len(RAW_SLOTS_A)] * SLOT_BYTES, "raw_a%d" % n, 1 if n == 0 else CH)
                s1 = ring.tile(
                    [P, CH, ND, PACK],
                    BF16,
                    name="s1_%d" % n,
                    offset=S1_SLOTS_A[n % len(S1_SLOTS_A)] * SLOT_BYTES,
                    align_bytes=64,
                )
                words_of_a(s1, raw, c in VECTOR_S1_A[ih])
                nc.vector.tensor_tensor(
                    out=ga[:, :, c * CH : (c + 1) * CH, :],
                    in0=s1[:].rearrange("p r d t -> p d r t"),
                    in1=mask_pit[:, i0 : i0 + CH, :].unsqueeze(1).to_broadcast([P, ND, CH, PACK]),
                    op=ALU.mult,
                )
            if ih == NI // IH - 1:
                gb0 = ring.tile([P, NG, JH, DBANK, PACK], BF16, name="gb0", offset=GB0_SLOT * SLOT_BYTES, align_bytes=64)
                for c in range(JH // CH):
                    raw = load(b_gated, c * CH, ring, RAW_SLOTS_B0[c] * SLOT_BYTES, "raw_b0_%d" % c)
                    words_of_b(gb0, c * CH, raw, c in VECTOR_S1_B[0])
            for d in range(ND):
                nc.vector.quantize_mx(
                    out=a_codes[:, d, ih * IH : (ih + 1) * IH].bitcast(FP8X4),
                    scales=a_scales[:, d, ih * IH : (ih + 1) * IH],
                    in_=ga[:, d, :, :].rearrange("p r t -> p (r t)"),
                )

        wb16_placed = small.tile([P, ND], BF16)
        nc.vector.tensor_copy(
            out=wb16_placed[:].rearrange("p (q g) -> p q g", q=DBANK),
            in_=wb16[:].rearrange("p (g q) -> p q g", q=DBANK),
        )
        wb_ps = psum.tile([P, P], BF16, tag="bank")
        nc.tensor.transpose(wb_ps[:], wb16_placed[:], ident[:])
        wb_col = small.tile([P, 2], F32)
        nc.vector.tensor_copy(out=wb_col[:], in_=wb_ps[:, 0:2])
        unplace = small.tile([P, P], F32)
        nc.vector.tensor_copy(
            out=unplace[:].rearrange("p (g q) -> p q g", q=DBANK),
            in_=ident_f32[:].rearrange("p (q g) -> p q g", q=DBANK),
        )

        t_sb0 = grp.tile([P, JH, ND], F32, name="t_sb0", offset=12 * SLOT_BYTES, align_bytes=64)
        t_sb = [t_sb0]

        def products(h, banks):
            for bank in banks:
                g0 = bank // DBANK * DBANK
                q = bank % DBANK
                acc = psum.tile([P, DBANK, JH, DBANK], F32, tag="bank")
                for s in range(DBANK):
                    d = DBANK * (g0 + s) + q
                    nc.tensor.matmul_mx(
                        out=acc[:, s, :, :].rearrange("p j c -> p (j c)"),
                        lhsT=a_codes[:, d, :].bitcast(FP8X4),
                        lhsT_scale=a_scales[:, d, :],
                        rhs=b_codes[h][:, g0 + s, :].bitcast(FP8X4),
                        rhs_scale=b_scales[h][:, g0 + s, :],
                        start=True,
                        stop=True,
                    )
                place = q * NG + g0
                nc.scalar.copy(
                    out=t_sb[h][:, :, place : place + DBANK], in_=acc[:, :, :, q].rearrange("p s j -> p j s")
                )

        b_codes = [
            grp.tile([P, NG, JH * DBANK], U32, name="b_codes%d" % h, offset=h * ND * JH * 5, align_bytes=64)
            for h in range(NJ // JH)
        ]
        b_scales = [
            grp.tile([P, NG, JH * DBANK], U8, name="b_scales%d" % h, offset=h * ND * JH * 5 + ND * JH * 4, align_bytes=64)
            for h in range(NJ // JH)
        ]
        for h in range(NJ // JH):
            if h == 0:
                gb = gb0
            else:
                gb = ring.tile([P, NG, JH, DBANK, PACK], BF16, name="gb1", offset=GB1_SLOT * SLOT_BYTES, align_bytes=64)
                for c in range(JH // CH):
                    if RAW_SLOTS_B1[c] is not None:
                        pool, offset = ring, RAW_SLOTS_B1[c] * SLOT_BYTES
                    else:
                        pool, offset = grp, ND * JH * 10 + c % 2 * SLOT_BYTES
                    raw = load(b_gated, h * JH + c * CH, pool, offset, "raw_b%d_%d" % (h, c))
                    words_of_b(gb, c * CH, raw, c in VECTOR_S1_B[h])
            gq = QW // (JH * DBANK * PACK)
            for g0 in range(0, NG, gq):
                nc.vector.quantize_mx(
                    out=b_codes[h][:, g0 : g0 + gq, :].rearrange("p g w -> p (g w)").bitcast(FP8X4),
                    scales=b_scales[h][:, g0 : g0 + gq, :].rearrange("p g w -> p (g w)"),
                    in_=gb[:, g0 : g0 + gq, :, :, :].rearrange("p g r q t -> p (g r q t)"),
                )
            if h == 0:
                products(0, range(ND // DBANK))
        t_sb1 = ring.tile([P, JH, ND], F32, name="t_sb1", offset=GB0_SLOT * SLOT_BYTES, align_bytes=64)
        t_sb.append(t_sb1)


        late_offset = [(GB0_SLOT + 6) * SLOT_BYTES]

        def late_tile(shape, name):
            size = 4
            for n in shape[1:]:
                size *= n
            t = ring.tile(shape, F32, name=name, offset=late_offset[0], align_bytes=64)
            late_offset[0] += (size + 63) // 64 * 64
            return t

        stats = [late_tile([P, JH // 2, 2, 3], "stats%d" % h) for h in range(NJ // JH)]
        rstd = [late_tile([P, JH // 2, 2], "rstd%d" % h) for h in range(NJ // JH)]

        def moments(h, k):
            for n in range(k * BATCH // 2, (k + 1) * BATCH // 2):
                nc.vector.bn_stats(
                    out=stats[h][:, n, :, :].rearrange("p e s -> p (e s)"),
                    in_=t_sb[h][:, 2 * n : 2 * n + 2, :].rearrange("p e d -> p d e"),
                )

        def root(h, k):
            ns = slice(k * BATCH // 2, (k + 1) * BATCH // 2)
            nc.scalar.activation(
                out=rstd[h][:, ns, :],
                in_=stats[h][:, ns, :, 2],
                func=ACT.Abs_reciprocal_sqrt,
                scale=1.0 / ND,
                bias=eps_t[:, 0:1],
            )

        def normalise(h, k):
            for j in range(k * BATCH, (k + 1) * BATCH):
                n, e = j // 2, j % 2
                nc.vector.tensor_scalar(
                    out=t_sb[h][:, j, :],
                    in0=t_sb[h][:, j, :],
                    scalar1=stats[h][:, n, e, 1:2],
                    scalar2=rstd[h][:, n, e : e + 1],
                    op0=ALU.subtract,
                    op1=ALU.mult,
                )

        turned = {}
        scaled = {}
        n_scaled = [0]

        def turn(h, g):
            bank = psum.tile([P, JG, P], F32, tag="bank")
            for n in range(JG):
                nc.tensor.transpose(bank[:, n, :], t_sb[h][:, g * JG + n, :], ident_f32[:])
            turned[h, g] = bank

        def gain_bias(h, g):
            n = n_scaled[0]
            n_scaled[0] += 1
            tile = ring.tile([P, JG, P], F32, name="scaled%d" % n, offset=4 * SLOT_BYTES + (n % SCALED_BUFS) * JG * P * 4, align_bytes=64)
            nc.scalar.activation(
                out=tile[:], in_=turned[h, g][:], func=ACT.Identity, scale=wb_col[:, 0:1], bias=wb_col[:, 1:2]
            )
            scaled[h, g] = tile

        def turn_back(h, g):
            for n in range(JG):
                nc.tensor.transpose(turned[h, g][:, n, :], scaled[h, g][:, n, :], unplace[:])

        def out_of_psum(copy, h, g):
            copy(out=t_sb[h][:, g * JG : (g + 1) * JG, :], in_=turned[h, g][:])

        def store(h, g0, g1):
            js = slice(g0 * JG, g1 * JG)
            nc.sync.dma_start(out=out[:, h * JH + js.start : h * JH + js.stop, :], in_=t_sb[h][:, js, :])

        n_banks = ND // DBANK
        on_vector = nc.vector.tensor_copy
        on_scalar = nc.scalar.copy

        with tc.manual_schedule(
            engines={mybir.EngineType.PE, mybir.EngineType.Activation, mybir.EngineType.DVE}
        ):
            products(1, range(0, 18))
            moments(0, 0)
            root(0, 0)
            products(1, range(18, 22))
            moments(0, 1)
            root(0, 1)
            normalise(0, 0)
            products(1, range(22, 27))
            moments(0, 2)
            root(0, 2)
            normalise(0, 1)
            products(1, range(27, n_banks))
            moments(0, 3)
            root(0, 3)
            normalise(0, 2)
            turn(0, 0)
            turn(0, 1)
            turn(0, 2)
            turn(0, 3)
            gain_bias(0, 0)
            turn_back(0, 0)
            gain_bias(0, 1)
            turn_back(0, 1)
            moments(1, 0)
            root(1, 0)
            normalise(0, 3)
            moments(1, 1)
            turn(0, 4)
            turn(0, 5)
            gain_bias(0, 2)
            turn_back(0, 2)
            gain_bias(0, 3)
            turn_back(0, 3)
            root(1, 1)
            normalise(1, 0)
            turn(0, 6)
            turn(0, 7)
            gain_bias(0, 4)
            turn_back(0, 4)
            out_of_psum(on_scalar, 0, 0)
            turn(1, 0)
            gain_bias(0, 5)
            turn_back(0, 5)
            out_of_psum(on_scalar, 0, 1)
            store(0, 0, 2)
            turn(1, 1)
            moments(1, 2)
            normalise(1, 1)
            root(1, 2)
            gain_bias(0, 6)
            turn_back(0, 6)
            gain_bias(0, 7)
            turn_back(0, 7)
            moments(1, 3)
            out_of_psum(on_scalar, 0, 2)
            turn(1, 2)
            root(1, 3)
            normalise(1, 2)
            gain_bias(1, 0)
            turn_back(1, 0)
            gain_bias(1, 1)
            turn_back(1, 1)
            normalise(1, 3)
            out_of_psum(on_vector, 0, 3)
            store(0, 2, 4)
            turn(1, 3)
            out_of_psum(on_vector, 0, 4)
            turn(1, 4)
            gain_bias(1, 2)
            turn_back(1, 2)
            gain_bias(1, 3)
            turn_back(1, 3)
            out_of_psum(on_vector, 0, 5)
            store(0, 4, 6)
            turn(1, 5)
            out_of_psum(on_vector, 0, 6)
            turn(1, 6)
            out_of_psum(on_vector, 0, 7)
            store(0, 6, 8)
            turn(1, 7)
            gain_bias(1, 4)
            turn_back(1, 4)
            gain_bias(1, 5)
            turn_back(1, 5)
            out_of_psum(on_vector, 1, 0)
            gain_bias(1, 6)
            turn_back(1, 6)
            gain_bias(1, 7)
            turn_back(1, 7)
            out_of_psum(on_vector, 1, 1)
            store(1, 0, 2)
            out_of_psum(on_vector, 1, 2)
            out_of_psum(on_scalar, 1, 3)
            store(1, 2, 4)
            out_of_psum(on_vector, 1, 4)
            out_of_psum(on_scalar, 1, 5)
            store(1, 4, 6)
            out_of_psum(on_vector, 1, 6)
            out_of_psum(on_scalar, 1, 7)
            store(1, 6, 8)
